import numpy as np
import ml_dtypes


def mxq(x, axis, fmt="e4m3"):
    dtype, down = {"e4m3": (ml_dtypes.float8_e4m3fn, 7), "e5m2": (ml_dtypes.float8_e5m2, 14)}[fmt]
    v = np.moveaxis(np.asarray(x, np.float32).astype(ml_dtypes.bfloat16).astype(np.float64), axis, -1)
    blocks = v.reshape(v.shape[:-1] + (-1, 32))
    amax = np.abs(blocks).max(-1, keepdims=True)
    byte = np.maximum(np.where(amax > 0, np.frexp(amax)[1] - 1 + 127, 0) - down, 1)
    scale = np.exp2(byte - 127.0)
    codes = (blocks / scale).astype(np.float32).astype(dtype).astype(np.float64)
    return np.moveaxis((codes * scale).reshape(v.shape), -1, axis)


WIDE = False


def mx_kscale(k):
    if not WIDE:
        return np.ones(k)
    levels = np.array([10, -10, 5, -5, 0])
    if k % 512:
        return np.exp2(np.random.permutation(np.resize(levels, k // 32))).repeat(32)
    a = np.empty((k // 512, 16))
    for p in range(k // 512):
        a[p, :8] = np.random.permutation(np.resize(levels, 8))
        for g in range(8):
            far = levels[np.abs(levels - a[p, g]) >= 10]
            a[p, g + 8] = far[np.random.randint(len(far))]
    return np.exp2(a.ravel()).repeat(32)


BF16 = ml_dtypes.bfloat16


def bf(x):
    return np.asarray(x, np.float32).astype(BF16)


def f64(x):
    return np.asarray(x).astype(np.float64)


B, S, HID, NH, HD, RD, RATIO = 4, 4096, 512, 8, 64, 32, 4
THETA = 10000.0
NW = S // RATIO
HALF = RD // 2


def rope_tables(positions):
    inv_freq = 1.0 / THETA ** (np.arange(HALF) / HALF)
    ang = positions[:, None] * inv_freq[None, :]
    return np.cos(ang), np.sin(ang)


def rope_interleaved(x, cos, sin):
    nope, rope = x[..., :-RD], x[..., -RD:]
    pr = rope.reshape(rope.shape[:-1] + (HALF, 2))
    a, b = pr[..., 0], pr[..., 1]
    new = np.stack([a * cos - b * sin, a * sin + b * cos], axis=-1).reshape(rope.shape)
    return np.concatenate([nope, new], axis=-1)


def remap(t, fill):
    cur = t[..., HD:]
    prev = np.concatenate([np.full((B, 1, RATIO, HD), fill), t[:, :-1, :, :HD]], axis=1)
    return np.concatenate([prev, cur], axis=2)


def pool_overlap(kv, gate, ape):
    kv_o = remap(kv.reshape(B, NW, RATIO, 2 * HD), 0.0)
    gate_o = remap(gate.reshape(B, NW, RATIO, 2 * HD) + ape, -np.inf)
    e = np.exp(gate_o - gate_o.max(axis=2, keepdims=True))
    w = e / e.sum(axis=2, keepdims=True)
    return (kv_o * w).sum(axis=2)


def setup_inputs():
    s = mx_kscale(HID)
    return {"hidden": bf(np.random.standard_normal((B, S, HID)) * s),
            "wkv": bf(np.random.standard_normal((HID, 2 * HD)) * 2.0 / np.sqrt(HID) / s[:, None]),
            "wgate": bf(np.random.standard_normal((HID, 2 * HD)) / np.sqrt(HID) / s[:, None]),
            "ape": bf(np.random.standard_normal((RATIO, 2 * HD)) * 0.5)}


def reference(hidden, wkv, wgate, ape):
    hq = mxq(f64(hidden), 2, "e4m3")
    kv = hq @ mxq(f64(wkv), 0, "e4m3")
    gate = hq @ mxq(f64(wgate), 0, "e4m3")
    pooled = pool_overlap(kv, gate, f64(ape))
    ck, sk = rope_tables(np.arange(NW) * RATIO)
    k_rot = rope_interleaved(pooled, ck, sk)
    return k_rot, pooled

@@ -1,0 +1,457 @@
+from contextlib import ExitStack
+import math
+
+import concourse.mybir as mybir
+from concourse.masks import make_identity
+
+F32 = mybir.dt.float32
+BF16 = mybir.dt.bfloat16
+I32 = mybir.dt.int32
+U32 = mybir.dt.uint32
+U8 = mybir.dt.uint8
+FP8X4 = mybir.dt.float8_e4m3fn_x4
+ALU = mybir.AluOpType
+ACT = mybir.ActivationFunctionType
+
+P = 128
+BATCH, SEQ, HID = 4, 4096, 512
+RATIO = 4
+HD = 64
+FEAT = 2 * HD
+ROPE = 32
+PAIRS = ROPE // 2
+THETA = 10000.0
+WPP = SEQ // RATIO // P
+WORDS = HID // 2
+GROUP = 4
+UNITS = BATCH * WPP
+LOADS_AHEAD = 7
+FLIPS_AHEAD = 3
+SLOTS = 2 * RATIO
+ENTRIES = WPP + 1
+ROW = ENTRIES * HD
+MINUS_BIG = -1.0e30
+ROUND_MAGIC = 1.5 * 2.0**23
+
+FLOPS = 2 * BATCH * SEQ * HID * 2 * FEAT
+
+
+def leading_bits(x, bits):
+    if x == 0.0:
+        return 0.0
+    step = 1.0
+    while abs(x) / step >= 2.0**bits:
+        step *= 2.0
+    while abs(x) / step < 2.0 ** (bits - 1):
+        step /= 2.0
+    return round(x / step) * step
+
+
+def quantise_weights(nc, const, wgate, wkv):
+    raw = const.tile([P, 4, 2, FEAT], BF16)
+    for m, w in enumerate((wgate, wkv)):
+        nc.sync.dma_start(out=raw[:, :, m, :], in_=w.rearrange("(q t) c -> q t c", t=4))
+    grouped = const.tile([P, 2, 2, HD, 4], BF16, align_bytes=64)
+    for a in range(2):
+        nc.vector.tensor_copy(
+            out=grouped[:, :, 1 - a, :, :],
+            in_=raw[:, :, :, a * HD : (a + 1) * HD].rearrange("q t m f -> q m f t"),
+        )
+    w_codes = const.tile([P, 2 * FEAT], U32, align_bytes=64)
+    w_scales = const.tile([P, 2 * FEAT], U8, align_bytes=64)
+    nc.vector.quantize_mx(
+        out=w_codes[:].bitcast(FP8X4),
+        scales=w_scales[:],
+        in_=grouped[:].rearrange("q m a f t -> q (m a f t)"),
+    )
+    return w_codes, w_scales
+
+
+def rope_angles(nc, const):
+    position_int = const.tile([P, WPP], I32)
+    nc.gpsimd.iota(position_int[:], pattern=[[RATIO, WPP]], base=0, channel_multiplier=RATIO * WPP)
+    position = const.tile([P, WPP], F32)
+    nc.vector.tensor_copy(out=position[:], in_=position_int[:])
+
+    angle_hi = const.tile([P, WPP, PAIRS], F32)
+    angle_lo = const.tile([P, WPP, PAIRS], F32)
+    for j in range(PAIRS):
+        frequency = 1.0 / THETA ** (j / PAIRS)
+        leading = leading_bits(frequency, 12)
+        for angle, factor in ((angle_hi, leading), (angle_lo, frequency - leading)):
+            nc.vector.tensor_scalar(
+                out=angle[:, :, j], in0=position[:], scalar1=factor, scalar2=None, op0=ALU.mult
+            )
+
+    turns = const.tile([P, WPP, PAIRS], F32)
+    nc.vector.tensor_tensor(out=turns[:], in0=angle_hi[:], in1=angle_lo[:], op=ALU.add)
+    nc.vector.tensor_scalar(
+        out=turns[:], in0=turns[:], scalar1=1.0 / (2.0 * math.pi), scalar2=ROUND_MAGIC,
+        op0=ALU.mult, op1=ALU.add,
+    )
+    nc.vector.tensor_scalar(
+        out=turns[:], in0=turns[:], scalar1=ROUND_MAGIC, scalar2=None, op0=ALU.subtract
+    )
+
+    piece_1 = leading_bits(2.0 * math.pi, 12)
+    piece_2 = leading_bits(2.0 * math.pi - piece_1, 12)
+    piece_3 = 2.0 * math.pi - piece_1 - piece_2
+    rest = const.tile([P, WPP, PAIRS], F32)
+    nc.vector.scalar_tensor_tensor(
+        out=rest[:], in0=turns[:], scalar=-piece_1, in1=angle_hi[:], op0=ALU.mult, op1=ALU.add
+    )
+    nc.vector.scalar_tensor_tensor(
+        out=rest[:], in0=turns[:], scalar=-piece_2, in1=rest[:], op0=ALU.mult, op1=ALU.add
+    )
+    nc.vector.tensor_tensor(out=rest[:], in0=rest[:], in1=angle_lo[:], op=ALU.add)
+    nc.vector.scalar_tensor_tensor(
+        out=rest[:], in0=turns[:], scalar=-piece_3, in1=rest[:], op0=ALU.mult, op1=ALU.add
+    )
+    return rest
+
+
+def rope_table(nc, const, rest):
+    sin_half = const.tile([P, WPP, PAIRS], F32)
+    sin_quarter = const.tile([P, WPP, PAIRS], F32)
+    nc.scalar.activation(out=sin_half[:], in_=rest[:], func=ACT.Sin, scale=0.5)
+    nc.scalar.activation(out=sin_quarter[:], in_=rest[:], func=ACT.Sin, scale=0.25)
+    cos_half = const.tile([P, WPP, PAIRS], F32)
+    nc.gpsimd.tensor_tensor(out=cos_half[:], in0=sin_quarter[:], in1=sin_quarter[:], op=ALU.mult)
+    nc.gpsimd.tensor_scalar(
+        out=cos_half[:], in0=cos_half[:], scalar1=-2.0, scalar2=1.0, op0=ALU.mult, op1=ALU.add
+    )
+    half_of_sin = const.tile([P, WPP, PAIRS], F32)
+    nc.gpsimd.tensor_tensor(out=half_of_sin[:], in0=sin_half[:], in1=cos_half[:], op=ALU.mult)
+    square = const.tile([P, WPP, PAIRS], F32)
+    nc.gpsimd.tensor_tensor(out=square[:], in0=sin_half[:], in1=sin_half[:], op=ALU.mult)
+
+    table = const.tile([P, WPP, 2, PAIRS, 2], F32)
+    for row, column in ((0, 0), (1, 1)):
+        nc.gpsimd.tensor_scalar(
+            out=table[:, :, row, :, column], in0=square[:], scalar1=-2.0, scalar2=1.0,
+            op0=ALU.mult, op1=ALU.add,
+        )
+    for row, column, sign in ((0, 1, -2.0), (1, 0, 2.0)):
+        nc.gpsimd.tensor_scalar(
+            out=table[:, :, row, :, column], in0=half_of_sin[:], scalar1=sign, scalar2=0.0,
+            op0=ALU.mult, op1=ALU.add,
+        )
+    return table
+
+
+def tile_deepseekv4attention_pa_t_kernel(tc, hidden, wkv, wgate, ape, out_0, out_1):
+    nc = tc.nc
+    with ExitStack() as ctx:
+        const = ctx.enter_context(tc.tile_pool(name="const", bufs=1))
+        tokens = ctx.enter_context(tc.tile_pool(name="tokens", bufs=LOADS_AHEAD - FLIPS_AHEAD + 1))
+        words = ctx.enter_context(tc.tile_pool(name="words", bufs=FLIPS_AHEAD + 1))
+        operand = ctx.enter_context(tc.tile_pool(name="operand", bufs=2))
+        sequence = ctx.enter_context(tc.tile_pool(name="sequence", bufs=2))
+        work = ctx.enter_context(tc.tile_pool(name="work", bufs=3))
+        psum_words = ctx.enter_context(tc.psum_pool(name="psum_words", bufs=2))
+        psum_proj = ctx.enter_context(tc.psum_pool(name="psum_proj", bufs=2))
+        psum_sums = ctx.enter_context(tc.psum_pool(name="psum_sums", bufs=1))
+
+        loaded = {}
+
+        def load(g):
+            j = (g - 1) % WPP
+            x = tokens.tile([P, RATIO * HID], BF16)
+            nc.sync.dma_start(
+                out=x[:],
+                in_=hidden[g // WPP].rearrange("(p t) k -> p (t k)", t=RATIO * WPP)[
+                    :, j * RATIO * HID : (j + 1) * RATIO * HID
+                ],
+            )
+            loaded[g] = x
+
+        load(0)
+        rest = rope_angles(nc, const)
+        w_codes, w_scales = quantise_weights(nc, const, wgate, wkv)
+
+        ape_bf16 = const.tile([P, RATIO, FEAT], BF16)
+        nc.sync.dma_start(
+            out=ape_bf16[:].rearrange("p r c -> p (r c)"),
+            in_=ape.rearrange("r c -> (r c)").partition_broadcast(P),
+        )
+        ape_f32 = const.tile([P, RATIO, 2, HD], F32)
+        for a in range(2):
+            nc.vector.tensor_copy(out=ape_f32[:, :, 1 - a, :], in_=ape_bf16[:, :, a * HD : (a + 1) * HD])
+
+        identity = const.tile([P, P], F32)
+        make_identity(nc, identity[:])
+        padded = const.tile([P, P + 1], F32)
+        nc.gpsimd.memset(padded[:, 0:1], 0.0)
+        make_identity(nc, padded[:, 1 : P + 1])
+        down = padded[:, 0:P]
+        no_window_before = const.tile([P, 1], F32)
+        nc.vector.tensor_scalar(
+            out=no_window_before[:], in0=identity[:, 0:1], scalar1=MINUS_BIG, scalar2=None,
+            op0=ALU.mult,
+        )
+
+        def by_slot(tape):
+            return tape[:, 0 : SLOTS * ROW].rearrange("p (s i f) -> p s i f", s=SLOTS, i=ENTRIES)
+
+        def unit_view(tape, j):
+            apart = RATIO * ROW + HD
+            both = tape[:, j * HD : j * HD + 2 * apart].rearrange("p (a x) -> p a x", a=2)
+            return both[:, :, 0 : RATIO * ROW].rearrange("p a (r y) -> p a r y", y=ROW)[:, :, :, 0:HD]
+
+        grouped_words_of, operand_of, products_of, tapes = {}, {}, {}, {}
+        moved_of, flipped_of, sums_of, table_of = {}, {}, {}, {}
+        top_of, inverse_of, pooled_of, products_rope_of = {}, {}, {}, {}
+
+        def flip_words(g):
+            x_words = loaded[g][:].bitcast(F32)
+            grouped = words.tile([P, RATIO * P, 4], BF16, align_bytes=64)
+            grouped_words = grouped[:].bitcast(F32)
+            for pair in range(RATIO // 2):
+                planes = psum_words.tile([P, 2, 2 * P], F32)
+                for r in (2 * pair, 2 * pair + 1):
+                    for u in range(2):
+                        nc.tensor.transpose(
+                            planes[:, u, (r % 2) * P : (r % 2 + 1) * P],
+                            x_words[:, r * WORDS + u : (r + 1) * WORDS : 2],
+                            identity[:],
+                        )
+                nc.scalar.copy(
+                    out=grouped_words[:, 2 * pair * P : 2 * (pair + 1) * P, :],
+                    in_=planes[:].rearrange("q u c -> q c u"),
+                )
+            grouped_words_of[g] = grouped
+
+        def quantise(g):
+            codes = operand.tile([P, RATIO * P], U32, align_bytes=64)
+            scales = operand.tile([P, RATIO * P], U8, align_bytes=64)
+            nc.vector.quantize_mx(
+                out=codes[:].bitcast(FP8X4),
+                scales=scales[:],
+                in_=grouped_words_of[g][:].rearrange("q c t -> q (c t)"),
+            )
+            operand_of[g] = (codes, scales)
+
+        def project(g):
+            codes, scales = operand_of[g]
+            gate_psum = psum_proj.tile([P, RATIO, 2, HD], F32)
+            kv_psum = psum_proj.tile([P, RATIO, 2, HD], F32)
+            for r in range(RATIO):
+                for psum, first in ((gate_psum, 0), (kv_psum, FEAT)):
+                    nc.tensor.matmul_mx(
+                        out=psum[:, r].rearrange("p a f -> p (a f)"),
+                        lhsT=codes[:, r * P : (r + 1) * P].bitcast(FP8X4),
+                        lhsT_scale=scales[:, r * P : (r + 1) * P],
+                        rhs=w_codes[:, first : first + FEAT].bitcast(FP8X4),
+                        rhs_scale=w_scales[:, first : first + FEAT],
+                        start=True,
+                        stop=True,
+                    )
+            products_of[g] = (gate_psum, kv_psum)
+
+        def land(g):
+            if g % WPP == 0:
+                gates = sequence.tile([P, (SLOTS + 1) * ROW], F32)
+                values = sequence.tile([P, (SLOTS + 1) * ROW], F32)
+                tapes[g // WPP] = (gates, values)
+            gates, values = tapes[g // WPP]
+            gate_psum, kv_psum = products_of[g]
+            j = (g - 1) % WPP
+            nc.vector.tensor_tensor(
+                out=unit_view(gates, j),
+                in0=gate_psum[:].rearrange("p r a f -> p a r f"),
+                in1=ape_f32[:].rearrange("p r a f -> p a r f"),
+                op=ALU.add,
+            )
+            nc.scalar.copy(
+                out=unit_view(values, j),
+                in_=kv_psum[:].rearrange("p r a f -> p a r f"),
+            )
+
+        def move_down(b):
+            moved = psum_sums.tile([P, 2, RATIO, HD], F32, tag="flipped")
+            for which in range(2):
+                nc.tensor.matmul(
+                    out=moved[:, which], lhsT=down, rhs=by_slot(tapes[b][which])[:, RATIO:SLOTS, WPP, :],
+                    start=True, stop=True,
+                )
+            moved_of[b] = moved
+
+        def take_moved(b):
+            gates, values = tapes[b]
+            moved = moved_of[b]
+            nc.vector.tensor_scalar(
+                out=by_slot(gates)[:, RATIO:SLOTS, 0, :], in0=moved[:, 0], scalar1=no_window_before[:, 0:1],
+                scalar2=None, op0=ALU.add,
+            )
+            nc.scalar.copy(out=by_slot(values)[:, RATIO:SLOTS, 0, :], in_=moved[:, 1])
+
+        groups = []
+        for b in range(BATCH):
+            sizes = [GROUP, GROUP] if b < BATCH - 1 else [GROUP, GROUP // 2, GROUP // 2]
+            for i, size in enumerate(sizes):
+                groups.append((b, sum(sizes[:i]), size))
+
+        def slots_of(n, which):
+            b, first, size = groups[n]
+            return by_slot(tapes[b][which])[:, :, first : first + size, :]
+
+        def top_of_4(n):
+            g = slots_of(n, 0)
+            top_4 = work.tile([P, 4, groups[n][2], HD], F32)
+            nc.vector.tensor_tensor(out=top_4[:], in0=g[:, 0:4], in1=g[:, 4:8], op=ALU.max)
+            top_of[n] = top_4
+
+        def top_of_2(n):
+            top_4 = top_of[n]
+            top_2 = work.tile([P, 2, groups[n][2], HD], F32)
+            nc.vector.tensor_tensor(out=top_2[:], in0=top_4[:, 0:2], in1=top_4[:, 2:4], op=ALU.max)
+            top_of[n] = top_2
+
+        def top_of_1(n):
+            top_2 = top_of[n]
+            top = work.tile([P, groups[n][2], HD], F32)
+            nc.vector.tensor_tensor(out=top[:], in0=top_2[:, 0], in1=top_2[:, 1], op=ALU.max)
+            top_of[n] = top
+
+        def subtract_top(n):
+            g = slots_of(n, 0)
+            nc.vector.tensor_tensor(
+                out=g, in0=g, in1=top_of[n][:].unsqueeze(1).to_broadcast([P, SLOTS, groups[n][2], HD]),
+                op=ALU.subtract,
+            )
+
+        def exponentiate(n):
+            nc.scalar.activation(out=slots_of(n, 0), in_=slots_of(n, 0), func=ACT.Exp)
+
+        def weigh(n):
+            nc.vector.tensor_tensor(
+                out=slots_of(n, 1), in0=slots_of(n, 1), in1=slots_of(n, 0), op=ALU.mult
+            )
+
+        def add_slots(n, which):
+            flipped = psum_sums.tile([P, groups[n][2] // 2, P], F32)
+            for two in range(groups[n][2] // 2):
+                for s in range(SLOTS):
+                    nc.tensor.matmul(
+                        out=flipped[:, two, :],
+                        lhsT=slots_of(n, which)[:, s, 2 * two : 2 * two + 2, :].rearrange("p w f -> p (w f)"),
+                        rhs=identity[:],
+                        is_transpose=True, start=(s == 0), stop=(s == SLOTS - 1),
+                    )
+            flipped_of[(n, which)] = flipped
+
+        def fetch_flipped(n, which):
+            flipped_sbuf = work.tile([P, groups[n][2] // 2, P], F32)
+            nc.scalar.copy(out=flipped_sbuf[:], in_=flipped_of[(n, which)][:])
+            flipped_of[(n, which)] = flipped_sbuf
+
+        def turn_back(n, which):
+            if which == 0:
+                sums = psum_sums.tile([P, 2, groups[n][2], HD], F32)
+                sums_of[n] = sums
+            for two in range(groups[n][2] // 2):
+                nc.tensor.transpose(
+                    sums_of[n][:, which, 2 * two : 2 * two + 2, :].rearrange("p w f -> p (w f)"),
+                    flipped_of[(n, which)][:, two, :],
+                    identity[:],
+                )
+
+        def rows_of(out, n):
+            b, first, size = groups[n]
+            return out[b].rearrange("(p w) f -> p w f", w=WPP)[:, first : first + size, :]
+
+        def invert(n):
+            inverse = work.tile([P, groups[n][2], HD], F32)
+            nc.vector.reciprocal(out=inverse[:], in_=sums_of[n][:, 0])
+            inverse_of[n] = inverse
+
+        def divide(n):
+            pooled = work.tile([P, groups[n][2], HD], F32)
+            nc.vector.tensor_tensor(
+                out=pooled[:], in0=sums_of[n][:, 1], in1=inverse_of[n][:], op=ALU.mult
+            )
+            nc.sync.dma_start(out=rows_of(out_1, n), in_=pooled[:])
+            nc.sync.dma_start(
+                out=rows_of(out_0, n)[:, :, 0 : HD - ROPE], in_=pooled[:, :, 0 : HD - ROPE]
+            )
+            pooled_of[n] = pooled
+
+        def rotate_products(n):
+            b, first, size = groups[n]
+            products = work.tile([P, size, 2, ROPE], F32)
+            nc.gpsimd.tensor_tensor(
+                out=products[:],
+                in0=pooled_of[n][:, :, HD - ROPE : HD].unsqueeze(2).to_broadcast([P, size, 2, ROPE]),
+                in1=table_of[0][:, first : first + size].rearrange("p w o j i -> p w o (j i)"),
+                op=ALU.mult,
+            )
+            products_rope_of[n] = products
+
+        def rotate_sums(n):
+            rotated = work.tile([P, groups[n][2], ROPE], F32)
+            pairs = products_rope_of[n][:].rearrange("p w o (j i) -> p w o j i", i=2)
+            nc.gpsimd.tensor_tensor(
+                out=rotated[:].rearrange("p w (j o) -> p w o j", o=2),
+                in0=pairs[:, :, :, :, 0],
+                in1=pairs[:, :, :, :, 1],
+                op=ALU.add,
+            )
+            nc.sync.dma_start(out=rows_of(out_0, n)[:, :, HD - ROPE : HD], in_=rotated[:])
+
+        def group_due(step):
+            for n, (b, first, size) in enumerate(groups):
+                if step == b * WPP + first + size:
+                    return n
+            return None
+
+        for g in range(1, LOADS_AHEAD - FLIPS_AHEAD):
+            load(g)
+        for step in range(-FLIPS_AHEAD, UNITS + 2 * GROUP + 1):
+            due = [group_due(step - k) for k in range(2 * GROUP + 1)]
+            if step + LOADS_AHEAD < UNITS:
+                load(step + LOADS_AHEAD)
+            if due[2] is not None:
+                exponentiate(due[2])
+            if due[4] is not None:
+                fetch_flipped(due[4], 0)
+            if due[5] is not None:
+                fetch_flipped(due[5], 1)
+            if step + FLIPS_AHEAD < UNITS:
+                flip_words(step + FLIPS_AHEAD)
+            if due[1] is not None:
+                top_of_1(due[1])
+            if 0 <= step + 1 < UNITS:
+                quantise(step + 1)
+                project(step + 1)
+            if 0 <= step < UNITS:
+                land(step)
+            if due[0] is not None:
+                top_of_4(due[0])
+            if due[7] is not None:
+                invert(due[7])
+            if due[8] is not None:
+                rotate_products(due[8])
+            if due[3] is not None:
+                weigh(due[3])
+            if due[1] is not None:
+                subtract_top(due[1])
+            if due[0] is not None:
+                top_of_2(due[0])
+            if due[7] is not None:
+                divide(due[7])
+            if due[8] is not None:
+                rotate_sums(due[8])
+            if step == 0:
+                table_of[0] = rope_table(nc, const, rest)
+            if 0 <= step - 1 < UNITS and (step - 1) % WPP == 0:
+                move_down((step - 1) // WPP)
+            if 0 <= step - 2 < UNITS and (step - 2) % WPP == 0:
+                take_moved((step - 2) // WPP)
+            if due[3] is not None:
+                add_slots(due[3], 0)
+            if due[4] is not None:
+                add_slots(due[4], 1)
+            if due[5] is not None:
+                turn_back(due[5], 0)
+            if due[6] is not None:
+                turn_back(due[6], 1)

@@ -12,6 +12,7 @@ U8 = mybir.dt.uint8
 FP8X4 = mybir.dt.float8_e4m3fn_x4
 ALU = mybir.AluOpType
 ACT = mybir.ActivationFunctionType
+ENGINES = mybir.EngineType
 
 P = 128
 BATCH, SEQ, HID = 4, 4096, 512
@@ -19,17 +20,15 @@ RATIO = 4
 HD = 64
 FEAT = 2 * HD
 ROPE = 32
-PAIRS = ROPE // 2
+HALF = ROPE // 2
 THETA = 10000.0
-WPP = SEQ // RATIO // P
+LOADS = 8
+UNITS = BATCH * SEQ // RATIO // P
+TWOS = UNITS // 2
+ROWS_PER_SEQ = P // BATCH
 WORDS = HID // 2
-GROUP = 4
-UNITS = BATCH * WPP
-LOADS_AHEAD = 7
-FLIPS_AHEAD = 3
 SLOTS = 2 * RATIO
-ENTRIES = WPP + 1
-ROW = ENTRIES * HD
+COLUMNS = RATIO * P
 MINUS_BIG = -1.0e30
 ROUND_MAGIC = 1.5 * 2.0**23
 
@@ -47,85 +46,115 @@ def leading_bits(x, bits):
     return round(x / step) * step
 
 
-def quantise_weights(nc, const, wgate, wkv):
+def load_weights(nc, const, wgate, wkv):
     raw = const.tile([P, 4, 2, FEAT], BF16)
     for m, w in enumerate((wgate, wkv)):
         nc.sync.dma_start(out=raw[:, :, m, :], in_=w.rearrange("(q t) c -> q t c", t=4))
-    grouped = const.tile([P, 2, 2, HD, 4], BF16, align_bytes=64)
-    for a in range(2):
-        nc.vector.tensor_copy(
-            out=grouped[:, :, 1 - a, :, :],
-            in_=raw[:, :, :, a * HD : (a + 1) * HD].rearrange("q t m f -> q m f t"),
-        )
-    w_codes = const.tile([P, 2 * FEAT], U32, align_bytes=64)
-    w_scales = const.tile([P, 2 * FEAT], U8, align_bytes=64)
-    nc.vector.quantize_mx(
-        out=w_codes[:].bitcast(FP8X4),
-        scales=w_scales[:],
-        in_=grouped[:].rearrange("q m a f t -> q (m a f t)"),
-    )
+    return raw
+
+
+def zero_weights(nc, const):
+    w_codes = const.tile([P, 2, 4 * HD], U32, align_bytes=64)
+    w_scales = const.tile([P, 2, 4 * HD], U8, align_bytes=64)
+    nc.gpsimd.memset(w_codes[:], 0)
+    nc.gpsimd.memset(w_scales[:], 0)
     return w_codes, w_scales
 
 
-def rope_angles(nc, const):
-    position_int = const.tile([P, WPP], I32)
-    nc.gpsimd.iota(position_int[:], pattern=[[RATIO, WPP]], base=0, channel_multiplier=RATIO * WPP)
-    position = const.tile([P, WPP], F32)
-    nc.vector.tensor_copy(out=position[:], in_=position_int[:])
+def quantise_weights(nc, const, raw, w_codes, w_scales):
+    grouped = const.tile([P, 2, 2, HD, 4], BF16, align_bytes=64)
+    for a in range(2):
+        nc.vector.tensor_copy(
+            out=grouped[:, :, 1 - a],
+            in_=raw[:, :, :, a * HD : (a + 1) * HD].rearrange("q t m f -> q m f t"),
+        )
+    for m in range(2):
+        nc.vector.quantize_mx(
+            out=w_codes[:, m, HD : 3 * HD].bitcast(FP8X4),
+            scales=w_scales[:, m, HD : 3 * HD],
+            in_=grouped[:, m].rearrange("q a f t -> q (a f t)"),
+        )
 
-    angle_hi = const.tile([P, WPP, PAIRS], F32)
-    angle_lo = const.tile([P, WPP, PAIRS], F32)
-    for j in range(PAIRS):
-        frequency = 1.0 / THETA ** (j / PAIRS)
+
+def window_positions(nc, const):
+    row_int = const.tile([P, 1], I32)
+    nc.gpsimd.iota(row_int[:], pattern=[[0, 1]], base=0, channel_multiplier=1)
+    position_int = const.tile([P, UNITS], I32)
+    nc.gpsimd.iota(
+        position_int[:], pattern=[[RATIO, UNITS]], base=0, channel_multiplier=RATIO * UNITS
+    )
+    row = const.tile([P, 1], F32)
+    nc.vector.tensor_copy(out=row[:], in_=row_int[:])
+    position = const.tile([P, UNITS], F32)
+    nc.vector.tensor_copy(out=position[:], in_=position_int[:])
+    back = const.tile([P, BATCH - 1], F32)
+    for b in range(1, BATCH):
+        nc.vector.tensor_scalar(
+            out=back[:, b - 1 : b], in0=row[:], scalar1=float(b * ROWS_PER_SEQ), scalar2=-float(SEQ),
+            op0=ALU.is_ge, op1=ALU.mult,
+        )
+    for b in range(1, BATCH):
+        nc.vector.tensor_scalar(
+            out=position[:], in0=position[:], scalar1=back[:, b - 1 : b], scalar2=None, op0=ALU.add
+        )
+    return position
+
+
+def rope_angles(nc, const, position):
+    angle_hi = const.tile([P, UNITS, HALF], F32)
+    angle_lo = const.tile([P, UNITS, HALF], F32)
+    for i in range(HALF):
+        frequency = 1.0 / THETA ** (i / HALF)
         leading = leading_bits(frequency, 12)
         for angle, factor in ((angle_hi, leading), (angle_lo, frequency - leading)):
             nc.vector.tensor_scalar(
-                out=angle[:, :, j], in0=position[:], scalar1=factor, scalar2=None, op0=ALU.mult
+                out=angle[:, :, i], in0=position[:], scalar1=factor, scalar2=None, op0=ALU.mult
             )
 
-    turns = const.tile([P, WPP, PAIRS], F32)
-    nc.vector.tensor_tensor(out=turns[:], in0=angle_hi[:], in1=angle_lo[:], op=ALU.add)
-    nc.vector.tensor_scalar(
+    turns = const.tile([P, UNITS, HALF], F32)
+    nc.gpsimd.tensor_tensor(out=turns[:], in0=angle_hi[:], in1=angle_lo[:], op=ALU.add)
+    nc.gpsimd.tensor_scalar(
         out=turns[:], in0=turns[:], scalar1=1.0 / (2.0 * math.pi), scalar2=ROUND_MAGIC,
         op0=ALU.mult, op1=ALU.add,
     )
-    nc.vector.tensor_scalar(
-        out=turns[:], in0=turns[:], scalar1=ROUND_MAGIC, scalar2=None, op0=ALU.subtract
+    nc.gpsimd.tensor_scalar(
+        out=turns[:], in0=turns[:], scalar1=1.0, scalar2=-ROUND_MAGIC, op0=ALU.mult, op1=ALU.add
     )
 
     piece_1 = leading_bits(2.0 * math.pi, 12)
     piece_2 = leading_bits(2.0 * math.pi - piece_1, 12)
     piece_3 = 2.0 * math.pi - piece_1 - piece_2
-    rest = const.tile([P, WPP, PAIRS], F32)
-    nc.vector.scalar_tensor_tensor(
-        out=rest[:], in0=turns[:], scalar=-piece_1, in1=angle_hi[:], op0=ALU.mult, op1=ALU.add
+    rest = const.tile([P, UNITS, HALF], F32)
+    whole = const.tile([P, UNITS, HALF], F32)
+    for piece, before in ((piece_1, angle_hi), (piece_2, rest)):
+        nc.gpsimd.tensor_scalar(
+            out=whole[:], in0=turns[:], scalar1=-piece, scalar2=0.0, op0=ALU.mult, op1=ALU.add
+        )
+        nc.gpsimd.tensor_tensor(out=rest[:], in0=whole[:], in1=before[:], op=ALU.add)
+    nc.gpsimd.tensor_tensor(out=rest[:], in0=rest[:], in1=angle_lo[:], op=ALU.add)
+    nc.gpsimd.tensor_scalar(
+        out=whole[:], in0=turns[:], scalar1=-piece_3, scalar2=0.0, op0=ALU.mult, op1=ALU.add
     )
-    nc.vector.scalar_tensor_tensor(
-        out=rest[:], in0=turns[:], scalar=-piece_2, in1=rest[:], op0=ALU.mult, op1=ALU.add
-    )
-    nc.vector.tensor_tensor(out=rest[:], in0=rest[:], in1=angle_lo[:], op=ALU.add)
-    nc.vector.scalar_tensor_tensor(
-        out=rest[:], in0=turns[:], scalar=-piece_3, in1=rest[:], op0=ALU.mult, op1=ALU.add
-    )
+    nc.gpsimd.tensor_tensor(out=rest[:], in0=whole[:], in1=rest[:], op=ALU.add)
     return rest
 
 
 def rope_table(nc, const, rest):
-    sin_half = const.tile([P, WPP, PAIRS], F32)
-    sin_quarter = const.tile([P, WPP, PAIRS], F32)
+    sin_half = const.tile([P, UNITS, HALF], F32)
+    sin_quarter = const.tile([P, UNITS, HALF], F32)
     nc.scalar.activation(out=sin_half[:], in_=rest[:], func=ACT.Sin, scale=0.5)
     nc.scalar.activation(out=sin_quarter[:], in_=rest[:], func=ACT.Sin, scale=0.25)
-    cos_half = const.tile([P, WPP, PAIRS], F32)
+    cos_half = const.tile([P, UNITS, HALF], F32)
     nc.gpsimd.tensor_tensor(out=cos_half[:], in0=sin_quarter[:], in1=sin_quarter[:], op=ALU.mult)
     nc.gpsimd.tensor_scalar(
         out=cos_half[:], in0=cos_half[:], scalar1=-2.0, scalar2=1.0, op0=ALU.mult, op1=ALU.add
     )
-    half_of_sin = const.tile([P, WPP, PAIRS], F32)
+    half_of_sin = const.tile([P, UNITS, HALF], F32)
     nc.gpsimd.tensor_tensor(out=half_of_sin[:], in0=sin_half[:], in1=cos_half[:], op=ALU.mult)
-    square = const.tile([P, WPP, PAIRS], F32)
+    square = const.tile([P, UNITS, HALF], F32)
     nc.gpsimd.tensor_tensor(out=square[:], in0=sin_half[:], in1=sin_half[:], op=ALU.mult)
 
-    table = const.tile([P, WPP, 2, PAIRS, 2], F32)
+    table = const.tile([P, UNITS, 2, HALF, 2], F32)
     for row, column in ((0, 0), (1, 1)):
         nc.gpsimd.tensor_scalar(
             out=table[:, :, row, :, column], in0=square[:], scalar1=-2.0, scalar2=1.0,
@@ -143,315 +172,321 @@ def tile_deepseekv4attention_pa_t_kernel(tc, hidden, wkv, wgate, ape, out_0, out
     nc = tc.nc
     with ExitStack() as ctx:
         const = ctx.enter_context(tc.tile_pool(name="const", bufs=1))
-        tokens = ctx.enter_context(tc.tile_pool(name="tokens", bufs=LOADS_AHEAD - FLIPS_AHEAD + 1))
-        words = ctx.enter_context(tc.tile_pool(name="words", bufs=FLIPS_AHEAD + 1))
-        operand = ctx.enter_context(tc.tile_pool(name="operand", bufs=2))
-        sequence = ctx.enter_context(tc.tile_pool(name="sequence", bufs=2))
+        tokens = ctx.enter_context(tc.tile_pool(name="tokens", bufs=LOADS))
+        words = ctx.enter_context(tc.tile_pool(name="words", bufs=6))
+        operand = ctx.enter_context(tc.tile_pool(name="operand", bufs=12))
+        gates_pool = ctx.enter_context(tc.tile_pool(name="gates_pool", bufs=5))
+        values_pool = ctx.enter_context(tc.tile_pool(name="values_pool", bufs=3))
         work = ctx.enter_context(tc.tile_pool(name="work", bufs=3))
-        psum_words = ctx.enter_context(tc.psum_pool(name="psum_words", bufs=2))
-        psum_proj = ctx.enter_context(tc.psum_pool(name="psum_proj", bufs=2))
+        psum_words = ctx.enter_context(tc.psum_pool(name="psum_words", bufs=3))
+        psum_gate = ctx.enter_context(tc.psum_pool(name="psum_gate", bufs=1))
+        psum_kv = ctx.enter_context(tc.psum_pool(name="psum_kv", bufs=1))
         psum_sums = ctx.enter_context(tc.psum_pool(name="psum_sums", bufs=1))
 
-        loaded = {}
+        tokens_of_row = hidden.rearrange("b s k -> (b s) k").rearrange("(p t) k -> p (t k)", p=P)
 
-        def load(g):
-            j = (g - 1) % WPP
+        order = [UNITS - 1] + list(range(UNITS - 1))
+        loaded, grouped_of, operand_of, products_of = {}, {}, {}, {}
+        gates_of, values_of, top_of, sums_of, inverse_of = {}, {}, {}, {}, {}
+        pooled_of, rotating_of = {}, {}
+
+        def load(i):
+            j = order[i]
             x = tokens.tile([P, RATIO * HID], BF16)
             nc.sync.dma_start(
-                out=x[:],
-                in_=hidden[g // WPP].rearrange("(p t) k -> p (t k)", t=RATIO * WPP)[
-                    :, j * RATIO * HID : (j + 1) * RATIO * HID
-                ],
+                out=x[:], in_=tokens_of_row[:, j * RATIO * HID : (j + 1) * RATIO * HID]
             )
-            loaded[g] = x
+            loaded[i] = x
 
         load(0)
-        rest = rope_angles(nc, const)
-        w_codes, w_scales = quantise_weights(nc, const, wgate, wkv)
-
-        ape_bf16 = const.tile([P, RATIO, FEAT], BF16)
-        nc.sync.dma_start(
-            out=ape_bf16[:].rearrange("p r c -> p (r c)"),
-            in_=ape.rearrange("r c -> (r c)").partition_broadcast(P),
-        )
-        ape_f32 = const.tile([P, RATIO, 2, HD], F32)
+        raw = load_weights(nc, const, wgate, wkv)
+        ape_rows = const.tile([P, P], BF16)
+        nc.gpsimd.memset(ape_rows[:], 0.0)
+        load(1)
+        load(2)
         for a in range(2):
-            nc.vector.tensor_copy(out=ape_f32[:, :, 1 - a, :], in_=ape_bf16[:, :, a * HD : (a + 1) * HD])
+            nc.sync.dma_start(
+                out=ape_rows[0:RATIO, a * HD : (a + 1) * HD], in_=ape[:, (1 - a) * HD : (2 - a) * HD]
+            )
+        nc.sync.dma_start(out=ape_rows[RATIO:SLOTS, :], in_=ape)
+        for i in range(3, LOADS):
+            load(i)
 
+        ctx.enter_context(
+            tc.manual_schedule(
+                engines={ENGINES.PE, ENGINES.Activation, ENGINES.DVE, ENGINES.Pool}
+            )
+        )
         identity = const.tile([P, P], F32)
         make_identity(nc, identity[:])
-        padded = const.tile([P, P + 1], F32)
-        nc.gpsimd.memset(padded[:, 0:1], 0.0)
-        make_identity(nc, padded[:, 1 : P + 1])
-        down = padded[:, 0:P]
-        no_window_before = const.tile([P, 1], F32)
-        nc.vector.tensor_scalar(
-            out=no_window_before[:], in0=identity[:, 0:1], scalar1=MINUS_BIG, scalar2=None,
-            op0=ALU.mult,
-        )
+        position = window_positions(nc, const)
+        w_codes, w_scales = zero_weights(nc, const)
+        rest = rope_angles(nc, const, position)
+        quantise_weights(nc, const, raw, w_codes, w_scales)
+        ape_f32 = const.tile([P, P], F32)
+        nc.vector.tensor_copy(out=ape_f32[:], in_=ape_rows[:])
+        ape_columns = const.tile([P, SLOTS], F32)
 
-        def by_slot(tape):
-            return tape[:, 0 : SLOTS * ROW].rearrange("p (s i f) -> p s i f", s=SLOTS, i=ENTRIES)
+        def turn_ape():
+            planes = psum_words.tile([P, 2, 2 * P], F32, tag="planes")
+            nc.tensor.transpose(planes[:, 0, 0:P], ape_f32[:], identity[:])
+            nc.scalar.copy(out=ape_columns[:], in_=planes[:, 0, 0:SLOTS])
 
-        def unit_view(tape, j):
-            apart = RATIO * ROW + HD
-            both = tape[:, j * HD : j * HD + 2 * apart].rearrange("p (a x) -> p a x", a=2)
-            return both[:, :, 0 : RATIO * ROW].rearrange("p a (r y) -> p a r y", y=ROW)[:, :, :, 0:HD]
+        def flip_words(i, half):
+            x_words = loaded[i][:].bitcast(F32)
+            planes = psum_words.tile([P, 2, 2 * P], F32, tag="planes")
+            for r in (2 * half, 2 * half + 1):
+                for u in range(2):
+                    nc.tensor.transpose(
+                        planes[:, u, (r % 2) * P : (r % 2 + 1) * P],
+                        x_words[:, r * WORDS + u : (r + 1) * WORDS : 2],
+                        identity[:],
+                    )
+            grouped_of[(i, half)] = planes
 
-        grouped_words_of, operand_of, products_of, tapes = {}, {}, {}, {}
-        moved_of, flipped_of, sums_of, table_of = {}, {}, {}, {}
-        top_of, inverse_of, pooled_of, products_rope_of = {}, {}, {}, {}
+        def group_words(i, half):
+            if half == 0:
+                grouped = words.tile([P, COLUMNS, 4], BF16, align_bytes=64)
+                grouped_of[i] = grouped
+            nc.scalar.copy(
+                out=grouped_of[i][:].bitcast(F32)[:, 2 * half * P : 2 * (half + 1) * P, :],
+                in_=grouped_of[(i, half)][:].rearrange("q u c -> q c u"),
+            )
 
-        def flip_words(g):
-            x_words = loaded[g][:].bitcast(F32)
-            grouped = words.tile([P, RATIO * P, 4], BF16, align_bytes=64)
-            grouped_words = grouped[:].bitcast(F32)
-            for pair in range(RATIO // 2):
-                planes = psum_words.tile([P, 2, 2 * P], F32)
-                for r in (2 * pair, 2 * pair + 1):
-                    for u in range(2):
-                        nc.tensor.transpose(
-                            planes[:, u, (r % 2) * P : (r % 2 + 1) * P],
-                            x_words[:, r * WORDS + u : (r + 1) * WORDS : 2],
-                            identity[:],
-                        )
-                nc.scalar.copy(
-                    out=grouped_words[:, 2 * pair * P : 2 * (pair + 1) * P, :],
-                    in_=planes[:].rearrange("q u c -> q c u"),
-                )
-            grouped_words_of[g] = grouped
-
-        def quantise(g):
-            codes = operand.tile([P, RATIO * P], U32, align_bytes=64)
-            scales = operand.tile([P, RATIO * P], U8, align_bytes=64)
+        def quantise(i):
+            pool = const if i == 0 else operand
+            codes = pool.tile([P, COLUMNS], U32, align_bytes=64)
+            scales = pool.tile([P, COLUMNS], U8, align_bytes=64)
             nc.vector.quantize_mx(
                 out=codes[:].bitcast(FP8X4),
                 scales=scales[:],
-                in_=grouped_words_of[g][:].rearrange("q c t -> q (c t)"),
+                in_=grouped_of[i][:].rearrange("q c t -> q (c t)"),
             )
-            operand_of[g] = (codes, scales)
+            operand_of[order[i]] = (codes, scales)
+            if i == 0:
+                move_on()
 
-        def project(g):
-            codes, scales = operand_of[g]
-            gate_psum = psum_proj.tile([P, RATIO, 2, HD], F32)
-            kv_psum = psum_proj.tile([P, RATIO, 2, HD], F32)
-            for r in range(RATIO):
-                for psum, first in ((gate_psum, 0), (kv_psum, FEAT)):
-                    nc.tensor.matmul_mx(
-                        out=psum[:, r].rearrange("p a f -> p (a f)"),
-                        lhsT=codes[:, r * P : (r + 1) * P].bitcast(FP8X4),
-                        lhsT_scale=scales[:, r * P : (r + 1) * P],
-                        rhs=w_codes[:, first : first + FEAT].bitcast(FP8X4),
-                        rhs_scale=w_scales[:, first : first + FEAT],
-                        start=True,
-                        stop=True,
-                    )
-            products_of[g] = (gate_psum, kv_psum)
+        def move_on():
+            codes, scales = operand_of[UNITS - 1]
+            moved_codes = const.tile([P, COLUMNS], U32, align_bytes=64)
+            moved_scales = const.tile([P, COLUMNS], U8, align_bytes=64)
+            for moved, source, dtype in ((moved_codes, codes, I32), (moved_scales, scales, U8)):
+                to = moved[:].bitcast(dtype).rearrange("q (r c) -> q r c", c=P)
+                of = source[:].bitcast(dtype).rearrange("q (r c) -> q r c", c=P)
+                nc.vector.tensor_copy(out=to[:, :, 1:P], in_=of[:, :, 0 : P - 1])
+                nc.vector.tensor_copy(out=to[:, :, 0:1], in_=of[:, :, P - 1 : P])
+            operand_of[-1] = (moved_codes, moved_scales)
 
-        def land(g):
-            if g % WPP == 0:
-                gates = sequence.tile([P, (SLOTS + 1) * ROW], F32)
-                values = sequence.tile([P, (SLOTS + 1) * ROW], F32)
-                tapes[g // WPP] = (gates, values)
-            gates, values = tapes[g // WPP]
-            gate_psum, kv_psum = products_of[g]
-            j = (g - 1) % WPP
-            nc.vector.tensor_tensor(
-                out=unit_view(gates, j),
-                in0=gate_psum[:].rearrange("p r a f -> p a r f"),
-                in1=ape_f32[:].rearrange("p r a f -> p a r f"),
-                op=ALU.add,
-            )
-            nc.scalar.copy(
-                out=unit_view(values, j),
-                in_=kv_psum[:].rearrange("p r a f -> p a r f"),
-            )
-
-        def move_down(b):
-            moved = psum_sums.tile([P, 2, RATIO, HD], F32, tag="flipped")
-            for which in range(2):
-                nc.tensor.matmul(
-                    out=moved[:, which], lhsT=down, rhs=by_slot(tapes[b][which])[:, RATIO:SLOTS, WPP, :],
-                    start=True, stop=True,
+        def project(n, m, half):
+            pool = (psum_gate, psum_kv)[m]
+            products = pool.tile([P, COLUMNS], F32, tag=f"half_{half}")
+            if half == 0:
+                passes = [(2 * n, HD)]
+            else:
+                passes = [(2 * n - 1, 2 * HD), (2 * n + 1, 0)]
+            for unit, first in passes:
+                codes, scales = operand_of[unit]
+                nc.tensor.matmul_mx(
+                    out=products[:],
+                    lhsT=w_codes[:, m, first : first + P].bitcast(FP8X4),
+                    lhsT_scale=w_scales[:, m, first : first + P],
+                    rhs=codes[:].bitcast(FP8X4),
+                    rhs_scale=scales[:],
+                    start=(unit == passes[0][0]),
+                    stop=(unit == passes[-1][0]),
                 )
-            moved_of[b] = moved
+            products_of[(n, m, half)] = products
 
-        def take_moved(b):
-            gates, values = tapes[b]
-            moved = moved_of[b]
-            nc.vector.tensor_scalar(
-                out=by_slot(gates)[:, RATIO:SLOTS, 0, :], in0=moved[:, 0], scalar1=no_window_before[:, 0:1],
-                scalar2=None, op0=ALU.add,
-            )
-            nc.scalar.copy(out=by_slot(values)[:, RATIO:SLOTS, 0, :], in_=moved[:, 1])
+        def half_of(tile, half):
+            return tile[:, half * RATIO : (half + 1) * RATIO, :]
 
-        groups = []
-        for b in range(BATCH):
-            sizes = [GROUP, GROUP] if b < BATCH - 1 else [GROUP, GROUP // 2, GROUP // 2]
-            for i, size in enumerate(sizes):
-                groups.append((b, sum(sizes[:i]), size))
-
-        def slots_of(n, which):
-            b, first, size = groups[n]
-            return by_slot(tapes[b][which])[:, :, first : first + size, :]
+        def land(n, half):
+            if n not in gates_of:
+                gates = gates_pool.tile([P, SLOTS, P], F32)
+                gates_of[n] = gates
+            for r in range(RATIO):
+                slot = half * RATIO + r
+                nc.scalar.activation(
+                    out=gates_of[n][:, slot, :],
+                    in_=products_of[(n, 0, half)][:, r * P : (r + 1) * P],
+                    func=ACT.Identity,
+                    bias=ape_columns[:, slot : slot + 1],
+                )
+            if n == 0 and half == 1:
+                nc.vector.memset(gates_of[n][0:HD, RATIO:SLOTS, 0:P:ROWS_PER_SEQ], MINUS_BIG)
 
         def top_of_4(n):
-            g = slots_of(n, 0)
-            top_4 = work.tile([P, 4, groups[n][2], HD], F32)
+            g = gates_of[n]
+            top_4 = work.tile([P, 4, P], F32)
             nc.vector.tensor_tensor(out=top_4[:], in0=g[:, 0:4], in1=g[:, 4:8], op=ALU.max)
             top_of[n] = top_4
 
         def top_of_2(n):
             top_4 = top_of[n]
-            top_2 = work.tile([P, 2, groups[n][2], HD], F32)
+            top_2 = work.tile([P, 2, P], F32)
             nc.vector.tensor_tensor(out=top_2[:], in0=top_4[:, 0:2], in1=top_4[:, 2:4], op=ALU.max)
             top_of[n] = top_2
 
         def top_of_1(n):
             top_2 = top_of[n]
-            top = work.tile([P, groups[n][2], HD], F32)
-            nc.vector.tensor_tensor(out=top[:], in0=top_2[:, 0], in1=top_2[:, 1], op=ALU.max)
+            top = work.tile([P, 1, P], F32)
+            nc.vector.tensor_tensor(out=top[:, 0], in0=top_2[:, 0], in1=top_2[:, 1], op=ALU.max)
             top_of[n] = top
 
         def subtract_top(n):
-            g = slots_of(n, 0)
+            g = gates_of[n]
             nc.vector.tensor_tensor(
-                out=g, in0=g, in1=top_of[n][:].unsqueeze(1).to_broadcast([P, SLOTS, groups[n][2], HD]),
-                op=ALU.subtract,
+                out=g[:], in0=g[:], in1=top_of[n][:].to_broadcast([P, SLOTS, P]), op=ALU.subtract
             )
 
-        def exponentiate(n):
-            nc.scalar.activation(out=slots_of(n, 0), in_=slots_of(n, 0), func=ACT.Exp)
+        def exponentiate(n, half):
+            g = half_of(gates_of[n], half)
+            nc.scalar.activation(out=g, in_=g, func=ACT.Exp)
 
-        def weigh(n):
+        def weigh(n, half):
+            if n not in values_of:
+                values = values_pool.tile([P, SLOTS, P], F32)
+                values_of[n] = values
             nc.vector.tensor_tensor(
-                out=slots_of(n, 1), in0=slots_of(n, 1), in1=slots_of(n, 0), op=ALU.mult
+                out=half_of(values_of[n], half),
+                in0=products_of[(n, 1, half)][:].rearrange("f (r p) -> f r p", r=RATIO),
+                in1=half_of(gates_of[n], half),
+                op=ALU.mult,
             )
 
         def add_slots(n, which):
-            flipped = psum_sums.tile([P, groups[n][2] // 2, P], F32)
-            for two in range(groups[n][2] // 2):
-                for s in range(SLOTS):
-                    nc.tensor.matmul(
-                        out=flipped[:, two, :],
-                        lhsT=slots_of(n, which)[:, s, 2 * two : 2 * two + 2, :].rearrange("p w f -> p (w f)"),
-                        rhs=identity[:],
-                        is_transpose=True, start=(s == 0), stop=(s == SLOTS - 1),
-                    )
-            flipped_of[(n, which)] = flipped
-
-        def fetch_flipped(n, which):
-            flipped_sbuf = work.tile([P, groups[n][2] // 2, P], F32)
-            nc.scalar.copy(out=flipped_sbuf[:], in_=flipped_of[(n, which)][:])
-            flipped_of[(n, which)] = flipped_sbuf
-
-        def turn_back(n, which):
             if which == 0:
-                sums = psum_sums.tile([P, 2, groups[n][2], HD], F32)
+                sums = psum_sums.tile([P, 2, P], F32)
                 sums_of[n] = sums
-            for two in range(groups[n][2] // 2):
-                nc.tensor.transpose(
-                    sums_of[n][:, which, 2 * two : 2 * two + 2, :].rearrange("p w f -> p (w f)"),
-                    flipped_of[(n, which)][:, two, :],
-                    identity[:],
+            tile = (gates_of, values_of)[which][n]
+            for s in range(SLOTS):
+                nc.tensor.matmul(
+                    out=sums_of[n][:, which, :], lhsT=tile[:, s, :], rhs=identity[:],
+                    is_transpose=True, start=(s == 0), stop=(s == SLOTS - 1),
                 )
 
-        def rows_of(out, n):
-            b, first, size = groups[n]
-            return out[b].rearrange("(p w) f -> p w f", w=WPP)[:, first : first + size, :]
+        batches = [(n, 2) for n in range(0, TWOS - 2, 2)] + [(TWOS - 2, 1), (TWOS - 1, 1)]
+        batch_of = {n: (first, count) for first, count in batches for n in range(first, first + count)}
 
         def invert(n):
-            inverse = work.tile([P, groups[n][2], HD], F32)
-            nc.vector.reciprocal(out=inverse[:], in_=sums_of[n][:, 0])
+            inverse = work.tile([P, P], F32)
+            nc.vector.reciprocal(out=inverse[:], in_=sums_of[n][:, 0, :])
             inverse_of[n] = inverse
 
         def divide(n):
-            pooled = work.tile([P, groups[n][2], HD], F32)
+            first, count = batch_of[n]
+            if n == first:
+                pooled = work.tile([P, count, 2, HD], F32)
+                pooled_of[first] = pooled
             nc.vector.tensor_tensor(
-                out=pooled[:], in0=sums_of[n][:, 1], in1=inverse_of[n][:], op=ALU.mult
+                out=pooled_of[first][:, n - first].rearrange("p w f -> p (w f)"),
+                in0=sums_of[n][:, 1, :],
+                in1=inverse_of[n][:],
+                op=ALU.mult,
             )
-            nc.sync.dma_start(out=rows_of(out_1, n), in_=pooled[:])
-            nc.sync.dma_start(
-                out=rows_of(out_0, n)[:, :, 0 : HD - ROPE], in_=pooled[:, :, 0 : HD - ROPE]
-            )
-            pooled_of[n] = pooled
 
-        def rotate_products(n):
-            b, first, size = groups[n]
+        def rows_of(out, first, count):
+            return out.rearrange("b w f -> (b w) f").rearrange("(p w) f -> p w f", p=P)[
+                :, 2 * first : 2 * (first + count), :
+            ]
+
+        def finish(n):
+            first, count = batch_of[n]
+            if n != first + count - 1:
+                return
+            size = 2 * count
+            pooled = pooled_of[first][:].rearrange("p i w f -> p (i w) f")
+            nc.sync.dma_start(out=rows_of(out_1, first, count), in_=pooled)
+            nc.sync.dma_start(
+                out=rows_of(out_0, first, count)[:, :, 0 : HD - ROPE], in_=pooled[:, :, 0 : HD - ROPE]
+            )
             products = work.tile([P, size, 2, ROPE], F32)
             nc.gpsimd.tensor_tensor(
                 out=products[:],
-                in0=pooled_of[n][:, :, HD - ROPE : HD].unsqueeze(2).to_broadcast([P, size, 2, ROPE]),
-                in1=table_of[0][:, first : first + size].rearrange("p w o j i -> p w o (j i)"),
+                in0=pooled[:, :, HD - ROPE : HD].unsqueeze(2).to_broadcast([P, size, 2, ROPE]),
+                in1=table_of[0][:, 2 * first : 2 * first + size].rearrange("p w o j i -> p w o (j i)"),
                 op=ALU.mult,
             )
-            products_rope_of[n] = products
-
-        def rotate_sums(n):
-            rotated = work.tile([P, groups[n][2], ROPE], F32)
-            pairs = products_rope_of[n][:].rearrange("p w o (j i) -> p w o j i", i=2)
+            rotated = work.tile([P, size, ROPE], F32)
+            pairs = products[:].rearrange("p w o (j i) -> p w o j i", i=2)
             nc.gpsimd.tensor_tensor(
                 out=rotated[:].rearrange("p w (j o) -> p w o j", o=2),
                 in0=pairs[:, :, :, :, 0],
                 in1=pairs[:, :, :, :, 1],
                 op=ALU.add,
             )
-            nc.sync.dma_start(out=rows_of(out_0, n)[:, :, HD - ROPE : HD], in_=rotated[:])
+            nc.sync.dma_start(
+                out=rows_of(out_0, first, count)[:, :, HD - ROPE : HD], in_=rotated[:]
+            )
 
-        def group_due(step):
-            for n, (b, first, size) in enumerate(groups):
-                if step == b * WPP + first + size:
-                    return n
-            return None
+        table_of = {}
 
-        for g in range(1, LOADS_AHEAD - FLIPS_AHEAD):
-            load(g)
-        for step in range(-FLIPS_AHEAD, UNITS + 2 * GROUP + 1):
-            due = [group_due(step - k) for k in range(2 * GROUP + 1)]
-            if step + LOADS_AHEAD < UNITS:
-                load(step + LOADS_AHEAD)
-            if due[2] is not None:
-                exponentiate(due[2])
-            if due[4] is not None:
-                fetch_flipped(due[4], 0)
-            if due[5] is not None:
-                fetch_flipped(due[5], 1)
-            if step + FLIPS_AHEAD < UNITS:
-                flip_words(step + FLIPS_AHEAD)
-            if due[1] is not None:
-                top_of_1(due[1])
-            if 0 <= step + 1 < UNITS:
-                quantise(step + 1)
-                project(step + 1)
-            if 0 <= step < UNITS:
-                land(step)
-            if due[0] is not None:
-                top_of_4(due[0])
-            if due[7] is not None:
-                invert(due[7])
-            if due[8] is not None:
-                rotate_products(due[8])
-            if due[3] is not None:
-                weigh(due[3])
-            if due[1] is not None:
-                subtract_top(due[1])
-            if due[0] is not None:
-                top_of_2(due[0])
-            if due[7] is not None:
-                divide(due[7])
-            if due[8] is not None:
-                rotate_sums(due[8])
-            if step == 0:
+        def units(first):
+            return [i if 0 <= i < UNITS else None for i in (first, first + 1)]
+
+        def pair(n):
+            return n if 0 <= n < TWOS else None
+
+        for k in range(-5, TWOS + 5):
+            flips, quantised = units(2 * (k + 3)), units(2 * (k + 2))
+            landing, topped, exped = pair(k), pair(k - 1), pair(k - 2)
+            weighed, divided, coming = pair(k - 3), pair(k - 4), pair(k + 1)
+            if k == -1:
+                turn_ape()
+            if topped is not None:
+                top_of_4(topped)
+            if divided is not None:
+                invert(divided)
+            if topped is not None:
+                top_of_2(topped)
+            if divided is not None:
+                divide(divided)
+            if topped is not None:
+                top_of_1(topped)
+            if quantised[0] is not None:
+                quantise(quantised[0])
+            if weighed is not None:
+                weigh(weighed, 0)
+            if quantised[1] is not None:
+                quantise(quantised[1])
+            if flips[0] is not None:
+                flip_words(flips[0], 0)
+                flip_words(flips[0], 1)
+            if flips[1] is not None:
+                flip_words(flips[1], 0)
+            if landing is not None:
+                land(landing, 0)
+                land(landing, 1)
+            if weighed is not None:
+                add_slots(weighed, 0)
+            if flips[0] is not None:
+                group_words(flips[0], 0)
+                group_words(flips[0], 1)
+            if weighed is not None:
+                weigh(weighed, 1)
+                add_slots(weighed, 1)
+            if exped is not None:
+                project(exped, 1, 1)
+            if flips[1] is not None:
+                flip_words(flips[1], 1)
+            if exped is not None:
+                project(exped, 1, 0)
+            if k == 1:
                 table_of[0] = rope_table(nc, const, rest)
-            if 0 <= step - 1 < UNITS and (step - 1) % WPP == 0:
-                move_down((step - 1) // WPP)
-            if 0 <= step - 2 < UNITS and (step - 2) % WPP == 0:
-                take_moved((step - 2) // WPP)
-            if due[3] is not None:
-                add_slots(due[3], 0)
-            if due[4] is not None:
-                add_slots(due[4], 1)
-            if due[5] is not None:
-                turn_back(due[5], 0)
-            if due[6] is not None:
-                turn_back(due[6], 1)
+            if exped is not None:
+                exponentiate(exped, 0)
+                exponentiate(exped, 1)
+            if topped is not None:
+                subtract_top(topped)
+            if flips[1] is not None:
+                group_words(flips[1], 0)
+            if coming is not None:
+                project(coming, 0, 0)
+                project(coming, 0, 1)
+            if flips[1] is not None:
+                group_words(flips[1], 1)
+            if divided is not None:
+                finish(divided)
+            for i in flips:
+                if i is not None and i + LOADS < UNITS:
+                    load(i + LOADS)

@@ -61,13 +61,17 @@ def zero_weights(nc, const):
     return w_codes, w_scales
 
 
-def quantise_weights(nc, const, raw, w_codes, w_scales):
+def group_weights(nc, const, raw):
     grouped = const.tile([P, 2, 2, HD, 4], BF16, align_bytes=64)
     for a in range(2):
         nc.vector.tensor_copy(
             out=grouped[:, :, 1 - a],
             in_=raw[:, :, :, a * HD : (a + 1) * HD].rearrange("q t m f -> q m f t"),
         )
+    return grouped
+
+
+def quantise_weights(nc, grouped, w_codes, w_scales):
     for m in range(2):
         nc.vector.quantize_mx(
             out=w_codes[:, m, HD : 3 * HD].bitcast(FP8X4),
@@ -112,60 +116,55 @@ def rope_angles(nc, const, position):
             )
 
     turns = const.tile([P, UNITS, HALF], F32)
-    nc.gpsimd.tensor_tensor(out=turns[:], in0=angle_hi[:], in1=angle_lo[:], op=ALU.add)
-    nc.gpsimd.tensor_scalar(
-        out=turns[:], in0=turns[:], scalar1=1.0 / (2.0 * math.pi), scalar2=ROUND_MAGIC,
-        op0=ALU.mult, op1=ALU.add,
-    )
-    nc.gpsimd.tensor_scalar(
-        out=turns[:], in0=turns[:], scalar1=1.0, scalar2=-ROUND_MAGIC, op0=ALU.mult, op1=ALU.add
-    )
-
+    rest = const.tile([P, UNITS, HALF], F32)
     piece_1 = leading_bits(2.0 * math.pi, 12)
     piece_2 = leading_bits(2.0 * math.pi - piece_1, 12)
     piece_3 = 2.0 * math.pi - piece_1 - piece_2
-    rest = const.tile([P, UNITS, HALF], F32)
-    whole = const.tile([P, UNITS, HALF], F32)
-    for piece, before in ((piece_1, angle_hi), (piece_2, rest)):
-        nc.gpsimd.tensor_scalar(
-            out=whole[:], in0=turns[:], scalar1=-piece, scalar2=0.0, op0=ALU.mult, op1=ALU.add
+
+    def subtract_turns(piece, before):
+        return lambda: nc.vector.scalar_tensor_tensor(
+            out=rest[:], in0=turns[:], scalar=-piece, in1=before[:], op0=ALU.mult, op1=ALU.add
         )
-        nc.gpsimd.tensor_tensor(out=rest[:], in0=whole[:], in1=before[:], op=ALU.add)
-    nc.gpsimd.tensor_tensor(out=rest[:], in0=rest[:], in1=angle_lo[:], op=ALU.add)
-    nc.gpsimd.tensor_scalar(
-        out=whole[:], in0=turns[:], scalar1=-piece_3, scalar2=0.0, op0=ALU.mult, op1=ALU.add
-    )
-    nc.gpsimd.tensor_tensor(out=rest[:], in0=whole[:], in1=rest[:], op=ALU.add)
-    return rest
+
+    pieces = [
+        lambda: nc.vector.tensor_scalar(
+            out=turns[:], in0=angle_hi[:], scalar1=1.0 / (2.0 * math.pi), scalar2=ROUND_MAGIC,
+            op0=ALU.mult, op1=ALU.add,
+        ),
+        lambda: nc.vector.tensor_scalar(
+            out=turns[:], in0=turns[:], scalar1=ROUND_MAGIC, scalar2=None, op0=ALU.subtract
+        ),
+        subtract_turns(piece_1, angle_hi),
+        subtract_turns(piece_2, rest),
+        lambda: nc.vector.tensor_tensor(out=rest[:], in0=rest[:], in1=angle_lo[:], op=ALU.add),
+        subtract_turns(piece_3, rest),
+    ]
+    return rest, pieces
 
 
 def rope_table(nc, const, rest):
     sin_half = const.tile([P, UNITS, HALF], F32)
     sin_quarter = const.tile([P, UNITS, HALF], F32)
-    nc.scalar.activation(out=sin_half[:], in_=rest[:], func=ACT.Sin, scale=0.5)
-    nc.scalar.activation(out=sin_quarter[:], in_=rest[:], func=ACT.Sin, scale=0.25)
-    cos_half = const.tile([P, UNITS, HALF], F32)
-    nc.gpsimd.tensor_tensor(out=cos_half[:], in0=sin_quarter[:], in1=sin_quarter[:], op=ALU.mult)
-    nc.gpsimd.tensor_scalar(
-        out=cos_half[:], in0=cos_half[:], scalar1=-2.0, scalar2=1.0, op0=ALU.mult, op1=ALU.add
-    )
-    half_of_sin = const.tile([P, UNITS, HALF], F32)
-    nc.gpsimd.tensor_tensor(out=half_of_sin[:], in0=sin_half[:], in1=cos_half[:], op=ALU.mult)
-    square = const.tile([P, UNITS, HALF], F32)
-    nc.gpsimd.tensor_tensor(out=square[:], in0=sin_half[:], in1=sin_half[:], op=ALU.mult)
-
-    table = const.tile([P, UNITS, 2, HALF, 2], F32)
-    for row, column in ((0, 0), (1, 1)):
-        nc.gpsimd.tensor_scalar(
-            out=table[:, :, row, :, column], in0=square[:], scalar1=-2.0, scalar2=1.0,
-            op0=ALU.mult, op1=ALU.add,
-        )
-    for row, column, sign in ((0, 1, -2.0), (1, 0, 2.0)):
-        nc.gpsimd.tensor_scalar(
-            out=table[:, :, row, :, column], in0=half_of_sin[:], scalar1=sign, scalar2=0.0,
-            op0=ALU.mult, op1=ALU.add,
-        )
-    return table
+    square_half = const.tile([P, UNITS, HALF], F32)
+    square_quarter = const.tile([P, UNITS, HALF], F32)
+    table = const.tile([P, UNITS, 2, HALF], F32)
+    activation = nc.scalar.activation
+    pieces = [
+        lambda: activation(out=sin_half[:], in_=rest[:], func=ACT.Sin, scale=0.5),
+        lambda: activation(out=sin_quarter[:], in_=rest[:], func=ACT.Sin, scale=0.25),
+        lambda: activation(out=square_half[:], in_=sin_half[:], func=ACT.Square),
+        lambda: activation(out=square_quarter[:], in_=sin_quarter[:], func=ACT.Square),
+        lambda: activation(
+            out=table[:, :, 0], in_=square_half[:], func=ACT.Copy, scale=-2.0, bias=1.0
+        ),
+        lambda: activation(
+            out=square_quarter[:], in_=square_quarter[:], func=ACT.Copy, scale=-4.0, bias=2.0
+        ),
+        lambda: nc.vector.tensor_tensor(
+            out=table[:, :, 1], in0=sin_half[:], in1=square_quarter[:], op=ALU.mult
+        ),
+    ]
+    return table, pieces
 
 
 def tile_deepseekv4attention_pa_t_kernel(tc, hidden, wkv, wgate, ape, out_0, out_1):
@@ -175,8 +174,8 @@ def tile_deepseekv4attention_pa_t_kernel(tc, hidden, wkv, wgate, ape, out_0, out
         tokens = ctx.enter_context(tc.tile_pool(name="tokens", bufs=LOADS))
         words = ctx.enter_context(tc.tile_pool(name="words", bufs=6))
         operand = ctx.enter_context(tc.tile_pool(name="operand", bufs=12))
-        gates_pool = ctx.enter_context(tc.tile_pool(name="gates_pool", bufs=5))
-        values_pool = ctx.enter_context(tc.tile_pool(name="values_pool", bufs=3))
+        gates_pool = ctx.enter_context(tc.tile_pool(name="gates_pool", bufs=7))
+        values_pool = ctx.enter_context(tc.tile_pool(name="values_pool", bufs=5))
         work = ctx.enter_context(tc.tile_pool(name="work", bufs=3))
         psum_words = ctx.enter_context(tc.psum_pool(name="psum_words", bufs=3))
         psum_gate = ctx.enter_context(tc.psum_pool(name="psum_gate", bufs=1))
@@ -198,12 +197,11 @@ def tile_deepseekv4attention_pa_t_kernel(tc, hidden, wkv, wgate, ape, out_0, out
             )
             loaded[i] = x
 
-        load(0)
+        for i in range(3):
+            load(i)
         raw = load_weights(nc, const, wgate, wkv)
         ape_rows = const.tile([P, P], BF16)
         nc.gpsimd.memset(ape_rows[:], 0.0)
-        load(1)
-        load(2)
         for a in range(2):
             nc.sync.dma_start(
                 out=ape_rows[0:RATIO, a * HD : (a + 1) * HD], in_=ape[:, (1 - a) * HD : (2 - a) * HD]
@@ -219,10 +217,12 @@ def tile_deepseekv4attention_pa_t_kernel(tc, hidden, wkv, wgate, ape, out_0, out
         )
         identity = const.tile([P, P], F32)
         make_identity(nc, identity[:])
+        nothing = const.tile([P, 1], F32)
+        nc.vector.memset(nothing[:], 0.0)
+        nc.scalar.activation(out=nothing[:], in_=nothing[:], func=ACT.Sin)
         position = window_positions(nc, const)
         w_codes, w_scales = zero_weights(nc, const)
-        rest = rope_angles(nc, const, position)
-        quantise_weights(nc, const, raw, w_codes, w_scales)
+        rest, angle_pieces = rope_angles(nc, const, position)
         ape_f32 = const.tile([P, P], F32)
         nc.vector.tensor_copy(out=ape_f32[:], in_=ape_rows[:])
         ape_columns = const.tile([P, SLOTS], F32)
@@ -264,7 +264,11 @@ def tile_deepseekv4attention_pa_t_kernel(tc, hidden, wkv, wgate, ape, out_0, out
             )
             operand_of[order[i]] = (codes, scales)
             if i == 0:
+                quantise_weights(nc, group_weights(nc, const, raw), w_codes, w_scales)
+            if i == 1:
                 move_on()
+            if angle_pieces:
+                angle_pieces.pop(0)()
 
         def move_on():
             codes, scales = operand_of[UNITS - 1]
@@ -304,7 +308,14 @@ def tile_deepseekv4attention_pa_t_kernel(tc, hidden, wkv, wgate, ape, out_0, out
             if n not in gates_of:
                 gates = gates_pool.tile([P, SLOTS, P], F32)
                 gates_of[n] = gates
-            for r in range(RATIO):
+            if n == 0:
+                nc.vector.tensor_tensor(
+                    out=half_of(gates_of[n], half),
+                    in0=products_of[(n, 0, half)][:].rearrange("f (r p) -> f r p", r=RATIO),
+                    in1=ape_columns[:, half * RATIO : (half + 1) * RATIO].unsqueeze(2).to_broadcast([P, RATIO, P]),
+                    op=ALU.add,
+                )
+            for r in range(RATIO if n > 0 else 0):
                 slot = half * RATIO + r
                 nc.scalar.activation(
                     out=gates_of[n][:, slot, :],
@@ -400,26 +411,30 @@ def tile_deepseekv4attention_pa_t_kernel(tc, hidden, wkv, wgate, ape, out_0, out
             nc.sync.dma_start(
                 out=rows_of(out_0, first, count)[:, :, 0 : HD - ROPE], in_=pooled[:, :, 0 : HD - ROPE]
             )
-            products = work.tile([P, size, 2, ROPE], F32)
-            nc.gpsimd.tensor_tensor(
-                out=products[:],
-                in0=pooled[:, :, HD - ROPE : HD].unsqueeze(2).to_broadcast([P, size, 2, ROPE]),
-                in1=table_of[0][:, 2 * first : 2 * first + size].rearrange("p w o j i -> p w o (j i)"),
-                op=ALU.mult,
-            )
+            products = work.tile([P, size, 2, HALF, 2], F32)
+            for o in range(2):
+                nc.gpsimd.tensor_tensor(
+                    out=products[:, :, o],
+                    in0=pooled[:, :, HD - ROPE : HD].rearrange("p w (j i) -> p w j i", i=2),
+                    in1=table_of[0][:, 2 * first : 2 * first + size, o]
+                    .unsqueeze(3)
+                    .to_broadcast([P, size, HALF, 2]),
+                    op=ALU.mult,
+                )
             rotated = work.tile([P, size, ROPE], F32)
-            pairs = products[:].rearrange("p w o (j i) -> p w o j i", i=2)
-            nc.gpsimd.tensor_tensor(
-                out=rotated[:].rearrange("p w (j o) -> p w o j", o=2),
-                in0=pairs[:, :, :, :, 0],
-                in1=pairs[:, :, :, :, 1],
-                op=ALU.add,
-            )
+            pairs = rotated[:].rearrange("p w (j i) -> p w j i", i=2)
+            for i, op in ((0, ALU.subtract), (1, ALU.add)):
+                nc.gpsimd.tensor_tensor(
+                    out=pairs[:, :, :, i],
+                    in0=products[:, :, 0, :, i],
+                    in1=products[:, :, 1, :, 1 - i],
+                    op=op,
+                )
             nc.sync.dma_start(
                 out=rows_of(out_0, first, count)[:, :, HD - ROPE : HD], in_=rotated[:]
             )
 
-        table_of = {}
+        table_of, table_pieces = {}, []
 
         def units(first):
             return [i if 0 <= i < UNITS else None for i in (first, first + 1)]
@@ -433,28 +448,29 @@ def tile_deepseekv4attention_pa_t_kernel(tc, hidden, wkv, wgate, ape, out_0, out
             weighed, divided, coming = pair(k - 3), pair(k - 4), pair(k + 1)
             if k == -1:
                 turn_ape()
+            if landing == 0:
+                land(landing, 0)
+                land(landing, 1)
             if topped is not None:
                 top_of_4(topped)
             if divided is not None:
                 invert(divided)
             if topped is not None:
                 top_of_2(topped)
-            if divided is not None:
-                divide(divided)
             if topped is not None:
                 top_of_1(topped)
             if quantised[0] is not None:
                 quantise(quantised[0])
+            if divided is not None:
+                divide(divided)
             if weighed is not None:
-                weigh(weighed, 0)
-            if quantised[1] is not None:
-                quantise(quantised[1])
+                weigh(weighed, 1)
             if flips[0] is not None:
                 flip_words(flips[0], 0)
                 flip_words(flips[0], 1)
             if flips[1] is not None:
                 flip_words(flips[1], 0)
-            if landing is not None:
+            if landing is not None and landing > 0:
                 land(landing, 0)
                 land(landing, 1)
             if weighed is not None:
@@ -463,16 +479,23 @@ def tile_deepseekv4attention_pa_t_kernel(tc, hidden, wkv, wgate, ape, out_0, out
                 group_words(flips[0], 0)
                 group_words(flips[0], 1)
             if weighed is not None:
-                weigh(weighed, 1)
+                weigh(weighed, 0)
                 add_slots(weighed, 1)
-            if exped is not None:
-                project(exped, 1, 1)
+            if quantised[1] is not None:
+                quantise(quantised[1])
             if flips[1] is not None:
                 flip_words(flips[1], 1)
+            if coming is not None:
+                project(coming, 0, 0)
+                project(coming, 0, 1)
             if exped is not None:
+                project(exped, 1, 1)
                 project(exped, 1, 0)
             if k == 1:
-                table_of[0] = rope_table(nc, const, rest)
+                table_of[0], table_pieces = rope_table(nc, const, rest)
+            for piece in table_pieces[:2]:
+                piece()
+            table_pieces = table_pieces[2:]
             if exped is not None:
                 exponentiate(exped, 0)
                 exponentiate(exped, 1)
@@ -480,10 +503,6 @@ def tile_deepseekv4attention_pa_t_kernel(tc, hidden, wkv, wgate, ape, out_0, out
                 subtract_top(topped)
             if flips[1] is not None:
                 group_words(flips[1], 0)
-            if coming is not None:
-                project(coming, 0, 0)
-                project(coming, 0, 1)
-            if flips[1] is not None:
                 group_words(flips[1], 1)
             if divided is not None:
                 finish(divided)

@@ -187,7 +187,7 @@ def tile_deepseekv4attention_pa_t_kernel(tc, hidden, wkv, wgate, ape, out_0, out
         order = [UNITS - 1] + list(range(UNITS - 1))
         loaded, grouped_of, operand_of, products_of = {}, {}, {}, {}
         gates_of, values_of, top_of, sums_of, inverse_of = {}, {}, {}, {}, {}
-        pooled_of, rotating_of = {}, {}
+        pooled_of, swapped_of, scaled_of = {}, {}, {}
 
         def load(i):
             j = order[i]
@@ -366,9 +366,12 @@ def tile_deepseekv4attention_pa_t_kernel(tc, hidden, wkv, wgate, ape, out_0, out
             )
 
         def add_slots(n, which):
-            if which == 0:
+            if which == 0 and n < TWOS - 7:
                 sums = psum_sums.tile([P, 2, P], F32)
                 sums_of[n] = sums
+            elif which == 0:
+                planes = psum_words.tile([P, 2, 2 * P], F32, tag="planes")
+                sums_of[n] = planes[:, :, 0:P]
             tile = (gates_of, values_of)[which][n]
             for s in range(SLOTS):
                 nc.tensor.matmul(
@@ -379,10 +382,33 @@ def tile_deepseekv4attention_pa_t_kernel(tc, hidden, wkv, wgate, ape, out_0, out
         batches = [(n, 2) for n in range(0, TWOS - 2, 2)] + [(TWOS - 2, 1), (TWOS - 1, 1)]
         batch_of = {n: (first, count) for first, count in batches for n in range(first, first + count)}
 
+        def keep_weights(n):
+            swapped = work.tile([P, 2, HD], F32)
+            for w in range(2):
+                nc.scalar.copy(out=swapped[:, 1 - w], in_=sums_of[n][:, 0, w * HD : (w + 1) * HD])
+            swapped_of[n] = swapped
+
+        def multiply_weights(n):
+            both = work.tile([P, 1, HD], F32)
+            nc.vector.tensor_tensor(
+                out=both[:, 0], in0=swapped_of[n][:, 0], in1=swapped_of[n][:, 1], op=ALU.mult
+            )
+            inverse_of[n] = both
+
         def invert(n):
-            inverse = work.tile([P, P], F32)
-            nc.vector.reciprocal(out=inverse[:], in_=sums_of[n][:, 0, :])
+            inverse = work.tile([P, 1, HD], F32)
+            nc.vector.reciprocal(out=inverse[:], in_=inverse_of[n][:])
             inverse_of[n] = inverse
+
+        def scale_values(n):
+            scaled = work.tile([P, 2, HD], F32)
+            nc.vector.tensor_tensor(
+                out=scaled[:],
+                in0=sums_of[n][:, 1, :].rearrange("p (w f) -> p w f", w=2),
+                in1=inverse_of[n][:].to_broadcast([P, 2, HD]),
+                op=ALU.mult,
+            )
+            scaled_of[n] = scaled
 
         def divide(n):
             first, count = batch_of[n]
@@ -390,10 +416,7 @@ def tile_deepseekv4attention_pa_t_kernel(tc, hidden, wkv, wgate, ape, out_0, out
                 pooled = work.tile([P, count, 2, HD], F32)
                 pooled_of[first] = pooled
             nc.vector.tensor_tensor(
-                out=pooled_of[first][:, n - first].rearrange("p w f -> p (w f)"),
-                in0=sums_of[n][:, 1, :],
-                in1=inverse_of[n][:],
-                op=ALU.mult,
+                out=pooled_of[first][:, n - first], in0=scaled_of[n][:], in1=swapped_of[n][:], op=ALU.mult
             )
 
         def rows_of(out, first, count):
@@ -442,29 +465,56 @@ def tile_deepseekv4attention_pa_t_kernel(tc, hidden, wkv, wgate, ape, out_0, out
         def pair(n):
             return n if 0 <= n < TWOS else None
 
-        for k in range(-5, TWOS + 5):
+        for k in range(-5, TWOS + 4):
             flips, quantised = units(2 * (k + 3)), units(2 * (k + 2))
-            landing, topped, exped = pair(k), pair(k - 1), pair(k - 2)
-            weighed, divided, coming = pair(k - 3), pair(k - 4), pair(k + 1)
+            landing, topped, exped, weighed = pair(k), pair(k - 1), pair(k - 2), pair(k - 3)
+            coming = pair(k + 1)
+            last = k >= TWOS
+            if not last:
+                summed, divided = [n for n in (pair(k - 4),) if n is not None], [pair(k - 5)]
+            elif k == TWOS:
+                summed, divided = [k - 4, k - 3], [k - 5]
+            else:
+                summed, divided = [n for n in (pair(k - 3),) if n is not None], [pair(k - 4)]
+            if k == TWOS + 1:
+                divided = [k - 5, k - 4]
+            divided = [n for n in divided if n is not None]
             if k == -1:
                 turn_ape()
+            if last and exped is not None and topped is None:
+                exponentiate(exped, 0)
+                exponentiate(exped, 1)
+            for n in divided:
+                keep_weights(n)
             if landing == 0:
                 land(landing, 0)
                 land(landing, 1)
+            if last and weighed is not None:
+                weigh(weighed, 1)
+                weigh(weighed, 0)
             if topped is not None:
                 top_of_4(topped)
-            if divided is not None:
-                invert(divided)
+            for n in divided:
+                multiply_weights(n)
             if topped is not None:
                 top_of_2(topped)
+            for n in divided:
+                invert(n)
             if topped is not None:
                 top_of_1(topped)
+            for n in divided:
+                scale_values(n)
+            if last and topped is not None:
+                subtract_top(topped)
             if quantised[0] is not None:
                 quantise(quantised[0])
-            if divided is not None:
-                divide(divided)
-            if weighed is not None:
+            for n in divided:
+                divide(n)
+            if weighed is not None and not last:
                 weigh(weighed, 1)
+                weigh(weighed, 0)
+            if quantised[1] is not None:
+                quantise(quantised[1])
             if flips[0] is not None:
                 flip_words(flips[0], 0)
                 flip_words(flips[0], 1)
@@ -473,22 +523,21 @@ def tile_deepseekv4attention_pa_t_kernel(tc, hidden, wkv, wgate, ape, out_0, out
             if landing is not None and landing > 0:
                 land(landing, 0)
                 land(landing, 1)
-            if weighed is not None:
-                add_slots(weighed, 0)
             if flips[0] is not None:
                 group_words(flips[0], 0)
                 group_words(flips[0], 1)
-            if weighed is not None:
-                weigh(weighed, 0)
-                add_slots(weighed, 1)
-            if quantised[1] is not None:
-                quantise(quantised[1])
             if flips[1] is not None:
                 flip_words(flips[1], 1)
+            if last and exped is not None:
+                project(exped, 1, 1)
+                project(exped, 1, 0)
+            for n in summed:
+                add_slots(n, 0)
+                add_slots(n, 1)
             if coming is not None:
                 project(coming, 0, 0)
                 project(coming, 0, 1)
-            if exped is not None:
+            if exped is not None and not last:
                 project(exped, 1, 1)
                 project(exped, 1, 0)
             if k == 1:
@@ -496,16 +545,16 @@ def tile_deepseekv4attention_pa_t_kernel(tc, hidden, wkv, wgate, ape, out_0, out
             for piece in table_pieces[:2]:
                 piece()
             table_pieces = table_pieces[2:]
-            if exped is not None:
+            if exped is not None and (topped is not None or not last):
                 exponentiate(exped, 0)
                 exponentiate(exped, 1)
-            if topped is not None:
+            if topped is not None and not last:
                 subtract_top(topped)
             if flips[1] is not None:
                 group_words(flips[1], 0)
                 group_words(flips[1], 1)
-            if divided is not None:
-                finish(divided)
+            for n in divided:
+                finish(n)
             for i in flips:
                 if i is not None and i + LOADS < UNITS:
                     load(i + LOADS)

@@ -64,9 +64,10 @@ def zero_weights(nc, const):
 def group_weights(nc, const, raw):
     grouped = const.tile([P, 2, 2, HD, 4], BF16, align_bytes=64)
     for a in range(2):
-        nc.vector.tensor_copy(
+        nc.gpsimd.tensor_scalar(
             out=grouped[:, :, 1 - a],
-            in_=raw[:, :, :, a * HD : (a + 1) * HD].rearrange("q t m f -> q m f t"),
+            in0=raw[:, :, :, a * HD : (a + 1) * HD].rearrange("q t m f -> q m f t"),
+            scalar1=1.0, scalar2=0.0, op0=ALU.mult, op1=ALU.add,
         )
     return grouped
 
@@ -80,88 +81,60 @@ def quantise_weights(nc, grouped, w_codes, w_scales):
         )
 
 
-def window_positions(nc, const):
-    row_int = const.tile([P, 1], I32)
-    nc.gpsimd.iota(row_int[:], pattern=[[0, 1]], base=0, channel_multiplier=1)
+def number_positions(nc, const):
     position_int = const.tile([P, UNITS], I32)
-    nc.gpsimd.iota(
-        position_int[:], pattern=[[RATIO, UNITS]], base=0, channel_multiplier=RATIO * UNITS
-    )
-    row = const.tile([P, 1], F32)
-    nc.vector.tensor_copy(out=row[:], in_=row_int[:])
-    position = const.tile([P, UNITS], F32)
-    nc.vector.tensor_copy(out=position[:], in_=position_int[:])
-    back = const.tile([P, BATCH - 1], F32)
-    for b in range(1, BATCH):
-        nc.vector.tensor_scalar(
-            out=back[:, b - 1 : b], in0=row[:], scalar1=float(b * ROWS_PER_SEQ), scalar2=-float(SEQ),
-            op0=ALU.is_ge, op1=ALU.mult,
+    for b in range(BATCH):
+        nc.gpsimd.iota(
+            position_int[b * ROWS_PER_SEQ : (b + 1) * ROWS_PER_SEQ, :],
+            pattern=[[RATIO, UNITS]], base=0, channel_multiplier=RATIO * UNITS,
         )
-    for b in range(1, BATCH):
-        nc.vector.tensor_scalar(
-            out=position[:], in0=position[:], scalar1=back[:, b - 1 : b], scalar2=None, op0=ALU.add
-        )
-    return position
+    return position_int
 
 
-def rope_angles(nc, const, position):
-    angle_hi = const.tile([P, UNITS, HALF], F32)
-    angle_lo = const.tile([P, UNITS, HALF], F32)
+def rope_turns(nc, const, position):
+    nearest = const.tile([P, HALF, UNITS], F32)
+    turns_hi = const.tile([P, HALF, UNITS], F32)
+    turns_lo = const.tile([P, HALF, UNITS], F32)
     for i in range(HALF):
-        frequency = 1.0 / THETA ** (i / HALF)
+        frequency = 1.0 / THETA ** (i / HALF) / (2.0 * math.pi)
         leading = leading_bits(frequency, 12)
-        for angle, factor in ((angle_hi, leading), (angle_lo, frequency - leading)):
-            nc.vector.tensor_scalar(
-                out=angle[:, :, i], in0=position[:], scalar1=factor, scalar2=None, op0=ALU.mult
-            )
-
-    turns = const.tile([P, UNITS, HALF], F32)
-    rest = const.tile([P, UNITS, HALF], F32)
-    piece_1 = leading_bits(2.0 * math.pi, 12)
-    piece_2 = leading_bits(2.0 * math.pi - piece_1, 12)
-    piece_3 = 2.0 * math.pi - piece_1 - piece_2
-
-    def subtract_turns(piece, before):
-        return lambda: nc.vector.scalar_tensor_tensor(
-            out=rest[:], in0=turns[:], scalar=-piece, in1=before[:], op0=ALU.mult, op1=ALU.add
-        )
-
-    pieces = [
-        lambda: nc.vector.tensor_scalar(
-            out=turns[:], in0=angle_hi[:], scalar1=1.0 / (2.0 * math.pi), scalar2=ROUND_MAGIC,
+        nc.vector.tensor_scalar(
+            out=nearest[:, i], in0=position[:], scalar1=frequency, scalar2=ROUND_MAGIC,
             op0=ALU.mult, op1=ALU.add,
+        )
+        nc.vector.tensor_scalar(
+            out=turns_hi[:, i], in0=position[:], scalar1=leading, scalar2=None, op0=ALU.mult
+        )
+        nc.scalar.activation(
+            out=turns_lo[:, i], in_=position[:], func=ACT.Copy, scale=frequency - leading
+        )
+    minus_rest = const.tile([P, HALF, UNITS], F32)
+    rest = const.tile([P, HALF, UNITS], F32)
+    pieces = [
+        lambda: nc.vector.scalar_tensor_tensor(
+            out=minus_rest[:], in0=nearest[:], scalar=ROUND_MAGIC, in1=turns_hi[:],
+            op0=ALU.subtract, op1=ALU.subtract,
         ),
-        lambda: nc.vector.tensor_scalar(
-            out=turns[:], in0=turns[:], scalar1=ROUND_MAGIC, scalar2=None, op0=ALU.subtract
+        lambda: nc.vector.tensor_tensor(
+            out=rest[:], in0=turns_lo[:], in1=minus_rest[:], op=ALU.subtract
         ),
-        subtract_turns(piece_1, angle_hi),
-        subtract_turns(piece_2, rest),
-        lambda: nc.vector.tensor_tensor(out=rest[:], in0=rest[:], in1=angle_lo[:], op=ALU.add),
-        subtract_turns(piece_3, rest),
     ]
     return rest, pieces
 
 
 def rope_table(nc, const, rest):
-    sin_half = const.tile([P, UNITS, HALF], F32)
-    sin_quarter = const.tile([P, UNITS, HALF], F32)
-    square_half = const.tile([P, UNITS, HALF], F32)
-    square_quarter = const.tile([P, UNITS, HALF], F32)
+    size = const.tile([P, HALF, UNITS], F32)
     table = const.tile([P, UNITS, 2, HALF], F32)
+    turn = 2.0 * math.pi
     activation = nc.scalar.activation
     pieces = [
-        lambda: activation(out=sin_half[:], in_=rest[:], func=ACT.Sin, scale=0.5),
-        lambda: activation(out=sin_quarter[:], in_=rest[:], func=ACT.Sin, scale=0.25),
-        lambda: activation(out=square_half[:], in_=sin_half[:], func=ACT.Square),
-        lambda: activation(out=square_quarter[:], in_=sin_quarter[:], func=ACT.Square),
         lambda: activation(
-            out=table[:, :, 0], in_=square_half[:], func=ACT.Copy, scale=-2.0, bias=1.0
+            out=table[:, :, 1], in_=rest[:].rearrange("p i j -> p j i"), func=ACT.Sin, scale=turn
         ),
+        lambda: activation(out=size[:], in_=rest[:], func=ACT.Abs),
         lambda: activation(
-            out=square_quarter[:], in_=square_quarter[:], func=ACT.Copy, scale=-4.0, bias=2.0
-        ),
-        lambda: nc.vector.tensor_tensor(
-            out=table[:, :, 1], in0=sin_half[:], in1=square_quarter[:], op=ALU.mult
+            out=table[:, :, 0], in_=size[:].rearrange("p i j -> p j i"), func=ACT.Sin, scale=-turn,
+            bias=math.pi / 2.0,
         ),
     ]
     return table, pieces
@@ -171,10 +144,11 @@ def tile_deepseekv4attention_pa_t_kernel(tc, hidden, wkv, wgate, ape, out_0, out
     nc = tc.nc
     with ExitStack() as ctx:
         const = ctx.enter_context(tc.tile_pool(name="const", bufs=1))
+        first = ctx.enter_context(tc.tile_pool(name="first", bufs=2))
         tokens = ctx.enter_context(tc.tile_pool(name="tokens", bufs=LOADS))
         words = ctx.enter_context(tc.tile_pool(name="words", bufs=6))
         operand = ctx.enter_context(tc.tile_pool(name="operand", bufs=12))
-        gates_pool = ctx.enter_context(tc.tile_pool(name="gates_pool", bufs=7))
+        gates_pool = ctx.enter_context(tc.tile_pool(name="gates_pool", bufs=6))
         values_pool = ctx.enter_context(tc.tile_pool(name="values_pool", bufs=5))
         work = ctx.enter_context(tc.tile_pool(name="work", bufs=3))
         psum_words = ctx.enter_context(tc.psum_pool(name="psum_words", bufs=3))
@@ -191,22 +165,26 @@ def tile_deepseekv4attention_pa_t_kernel(tc, hidden, wkv, wgate, ape, out_0, out
 
         def load(i):
             j = order[i]
-            x = tokens.tile([P, RATIO * HID], BF16)
-            nc.sync.dma_start(
-                out=x[:], in_=tokens_of_row[:, j * RATIO * HID : (j + 1) * RATIO * HID]
-            )
-            loaded[i] = x
+            pieces = 2 if i == 0 else 1
+            width = RATIO * HID // pieces
+            loaded[i] = []
+            for h in range(pieces):
+                if i == 0:
+                    x = first.tile([P, width], BF16)
+                else:
+                    x = tokens.tile([P, width], BF16)
+                begin = j * RATIO * HID + h * width
+                nc.sync.dma_start(out=x[:], in_=tokens_of_row[:, begin : begin + width])
+                loaded[i] += [(x, r * HID) for r in range(RATIO // pieces)]
 
-        for i in range(3):
-            load(i)
+        load(0)
+        load(1)
         raw = load_weights(nc, const, wgate, wkv)
-        ape_rows = const.tile([P, P], BF16)
+        load(2)
+        position_int = number_positions(nc, const)
+        ape_rows = const.tile([P, FEAT], BF16)
         nc.gpsimd.memset(ape_rows[:], 0.0)
-        for a in range(2):
-            nc.sync.dma_start(
-                out=ape_rows[0:RATIO, a * HD : (a + 1) * HD], in_=ape[:, (1 - a) * HD : (2 - a) * HD]
-            )
-        nc.sync.dma_start(out=ape_rows[RATIO:SLOTS, :], in_=ape)
+        nc.sync.dma_start(out=ape_rows[0:RATIO, :], in_=ape)
         for i in range(3, LOADS):
             load(i)
 
@@ -215,31 +193,43 @@ def tile_deepseekv4attention_pa_t_kernel(tc, hidden, wkv, wgate, ape, out_0, out
                 engines={ENGINES.PE, ENGINES.Activation, ENGINES.DVE, ENGINES.Pool}
             )
         )
+        position = const.tile([P, UNITS], F32)
+        nc.vector.tensor_copy(out=position[:], in_=position_int[:])
         identity = const.tile([P, P], F32)
         make_identity(nc, identity[:])
         nothing = const.tile([P, 1], F32)
         nc.vector.memset(nothing[:], 0.0)
         nc.scalar.activation(out=nothing[:], in_=nothing[:], func=ACT.Sin)
-        position = window_positions(nc, const)
         w_codes, w_scales = zero_weights(nc, const)
-        rest, angle_pieces = rope_angles(nc, const, position)
-        ape_f32 = const.tile([P, P], F32)
-        nc.vector.tensor_copy(out=ape_f32[:], in_=ape_rows[:])
+        rest, turn_pieces = rope_turns(nc, const, position)
+        table, table_pieces = rope_table(nc, const, rest)
+        ape_f32 = const.tile([P, 2, FEAT], F32)
         ape_columns = const.tile([P, SLOTS], F32)
+
+        def spread_ape():
+            for a in range(2):
+                nc.gpsimd.tensor_copy(
+                    out=ape_f32[:, 0, (1 - a) * HD : (2 - a) * HD], in_=ape_rows[:, a * HD : (a + 1) * HD]
+                )
+            nc.gpsimd.tensor_copy(out=ape_f32[:, 1], in_=ape_rows[:])
 
         def turn_ape():
             planes = psum_words.tile([P, 2, 2 * P], F32, tag="planes")
-            nc.tensor.transpose(planes[:, 0, 0:P], ape_f32[:], identity[:])
-            nc.scalar.copy(out=ape_columns[:], in_=planes[:, 0, 0:SLOTS])
+            for half in range(2):
+                nc.tensor.transpose(planes[:, half, 0:P], ape_f32[:, half], identity[:])
+            nc.scalar.copy(
+                out=ape_columns[:].rearrange("p (h r) -> p h r", h=2), in_=planes[:, :, 0:RATIO]
+            )
 
         def flip_words(i, half):
-            x_words = loaded[i][:].bitcast(F32)
             planes = psum_words.tile([P, 2, 2 * P], F32, tag="planes")
             for r in (2 * half, 2 * half + 1):
+                x, begin = loaded[i][r]
+                x_words = x[:, begin : begin + HID].bitcast(F32)
                 for u in range(2):
                     nc.tensor.transpose(
                         planes[:, u, (r % 2) * P : (r % 2 + 1) * P],
-                        x_words[:, r * WORDS + u : (r + 1) * WORDS : 2],
+                        x_words[:, u : WORDS : 2],
                         identity[:],
                     )
             grouped_of[(i, half)] = planes
@@ -263,22 +253,19 @@ def tile_deepseekv4attention_pa_t_kernel(tc, hidden, wkv, wgate, ape, out_0, out
                 in_=grouped_of[i][:].rearrange("q c t -> q (c t)"),
             )
             operand_of[order[i]] = (codes, scales)
-            if i == 0:
-                quantise_weights(nc, group_weights(nc, const, raw), w_codes, w_scales)
-            if i == 1:
-                move_on()
-            if angle_pieces:
-                angle_pieces.pop(0)()
 
         def move_on():
             codes, scales = operand_of[UNITS - 1]
             moved_codes = const.tile([P, COLUMNS], U32, align_bytes=64)
             moved_scales = const.tile([P, COLUMNS], U8, align_bytes=64)
-            for moved, source, dtype in ((moved_codes, codes, I32), (moved_scales, scales, U8)):
-                to = moved[:].bitcast(dtype).rearrange("q (r c) -> q r c", c=P)
-                of = source[:].bitcast(dtype).rearrange("q (r c) -> q r c", c=P)
-                nc.vector.tensor_copy(out=to[:, :, 1:P], in_=of[:, :, 0 : P - 1])
-                nc.vector.tensor_copy(out=to[:, :, 0:1], in_=of[:, :, P - 1 : P])
+            moves = ((moved_codes, codes, I32), (moved_scales, scales, U8))
+            for to_columns, of_columns in (((1, P), (0, P - 1)), ((0, 1), (P - 1, P))):
+                for moved, source, dtype in moves:
+                    to = moved[:].bitcast(dtype).rearrange("q (r c) -> q r c", c=P)
+                    of = source[:].bitcast(dtype).rearrange("q (r c) -> q r c", c=P)
+                    nc.vector.tensor_copy(
+                        out=to[:, :, slice(*to_columns)], in_=of[:, :, slice(*of_columns)]
+                    )
             operand_of[-1] = (moved_codes, moved_scales)
 
         def project(n, m, half):
@@ -366,7 +353,7 @@ def tile_deepseekv4attention_pa_t_kernel(tc, hidden, wkv, wgate, ape, out_0, out
             )
 
         def add_slots(n, which):
-            if which == 0 and n < TWOS - 7:
+            if which == 0 and n < TWOS - 5:
                 sums = psum_sums.tile([P, 2, P], F32)
                 sums_of[n] = sums
             elif which == 0:
@@ -439,7 +426,7 @@ def tile_deepseekv4attention_pa_t_kernel(tc, hidden, wkv, wgate, ape, out_0, out
                 nc.gpsimd.tensor_tensor(
                     out=products[:, :, o],
                     in0=pooled[:, :, HD - ROPE : HD].rearrange("p w (j i) -> p w j i", i=2),
-                    in1=table_of[0][:, 2 * first : 2 * first + size, o]
+                    in1=table[:, 2 * first : 2 * first + size, o]
                     .unsqueeze(3)
                     .to_broadcast([P, size, HALF, 2]),
                     op=ALU.mult,
@@ -457,104 +444,110 @@ def tile_deepseekv4attention_pa_t_kernel(tc, hidden, wkv, wgate, ape, out_0, out
                 out=rows_of(out_0, first, count)[:, :, HD - ROPE : HD], in_=rotated[:]
             )
 
-        table_of, table_pieces = {}, []
-
-        def units(first):
-            return [i if 0 <= i < UNITS else None for i in (first, first + 1)]
-
         def pair(n):
             return n if 0 <= n < TWOS else None
 
-        for k in range(-5, TWOS + 4):
-            flips, quantised = units(2 * (k + 3)), units(2 * (k + 2))
-            landing, topped, exped, weighed = pair(k), pair(k - 1), pair(k - 2), pair(k - 3)
-            coming = pair(k + 1)
-            last = k >= TWOS
-            if not last:
-                summed, divided = [n for n in (pair(k - 4),) if n is not None], [pair(k - 5)]
-            elif k == TWOS:
-                summed, divided = [k - 4, k - 3], [k - 5]
-            else:
-                summed, divided = [n for n in (pair(k - 3),) if n is not None], [pair(k - 4)]
+        def flip_and_group(i):
+            for half in range(2):
+                flip_words(i, half)
+                group_words(i, half)
+
+        weights = group_weights(nc, const, raw)
+        spread_ape()
+        for i in range(3):
+            flip_and_group(i)
+        turn_pieces[0]()
+        quantise(0)
+        turn_pieces[1]()
+        move_on()
+        quantise_weights(nc, weights, w_codes, w_scales)
+        quantise(1)
+        quantise(2)
+        flip_and_group(3)
+        turn_ape()
+        project(0, 0, 0)
+        project(0, 0, 1)
+        table_pieces[0]()
+        land(0, 0)
+        quantise(3)
+        land(0, 1)
+        flip_and_group(4)
+        table_pieces[1]()
+        table_pieces[2]()
+        for i in range(5):
+            load(i + LOADS)
+
+        for k in range(TWOS + 3):
+            landing, coming, exped, weighed = pair(k), pair(k + 1), pair(k - 1), pair(k - 2)
+            flips = [i for i in (2 * k + 5, 2 * k + 6) if i < UNITS]
+            quantised = [i for i in (2 * k + 4, 2 * k + 5) if i < UNITS]
+            summed, divided = pair(k - 3), pair(k - 4)
+            summed = [] if summed is None else [summed]
+            divided = [] if divided is None else [divided]
+            if k == TWOS + 2:
+                divided = [k - 4, k - 3]
+                summed = []
             if k == TWOS + 1:
-                divided = [k - 5, k - 4]
-            divided = [n for n in divided if n is not None]
-            if k == -1:
-                turn_ape()
-            if last and exped is not None and topped is None:
-                exponentiate(exped, 0)
-                exponentiate(exped, 1)
+                summed = [k - 3, k - 2]
+
             for n in divided:
                 keep_weights(n)
-            if landing == 0:
-                land(landing, 0)
-                land(landing, 1)
-            if last and weighed is not None:
-                weigh(weighed, 1)
-                weigh(weighed, 0)
-            if topped is not None:
-                top_of_4(topped)
-            for n in divided:
-                multiply_weights(n)
-            if topped is not None:
-                top_of_2(topped)
-            for n in divided:
-                invert(n)
-            if topped is not None:
-                top_of_1(topped)
-            for n in divided:
-                scale_values(n)
-            if last and topped is not None:
-                subtract_top(topped)
-            if quantised[0] is not None:
-                quantise(quantised[0])
-            for n in divided:
-                divide(n)
-            if weighed is not None and not last:
-                weigh(weighed, 1)
-                weigh(weighed, 0)
-            if quantised[1] is not None:
-                quantise(quantised[1])
-            if flips[0] is not None:
-                flip_words(flips[0], 0)
-                flip_words(flips[0], 1)
-            if flips[1] is not None:
-                flip_words(flips[1], 0)
             if landing is not None and landing > 0:
                 land(landing, 0)
                 land(landing, 1)
-            if flips[0] is not None:
+            for n in divided:
+                multiply_weights(n)
+            if exped is not None:
+                subtract_top(exped)
+            for n in divided:
+                invert(n)
+            if landing == 0:
+                top_of_4(landing)
+            if quantised:
+                quantise(quantised[0])
+            for n in divided:
+                scale_values(n)
+            if landing is not None and landing > 0:
+                top_of_4(landing)
+            for n in divided:
+                divide(n)
+            if weighed is not None:
+                weigh(weighed, 1)
+            if landing is not None:
+                top_of_2(landing)
+            if weighed is not None:
+                weigh(weighed, 0)
+            if landing is not None:
+                top_of_1(landing)
+            if flips:
+                flip_words(flips[0], 0)
+                flip_words(flips[0], 1)
                 group_words(flips[0], 0)
                 group_words(flips[0], 1)
-            if flips[1] is not None:
+            if k < 3 and coming is not None:
+                project(coming, 0, 0)
+                project(coming, 0, 1)
+            if len(flips) > 1:
+                flip_words(flips[1], 0)
                 flip_words(flips[1], 1)
-            if last and exped is not None:
-                project(exped, 1, 1)
-                project(exped, 1, 0)
+            if len(quantised) > 1:
+                quantise(quantised[1])
             for n in summed:
                 add_slots(n, 0)
                 add_slots(n, 1)
-            if coming is not None:
+            if k >= 3 and coming is not None:
                 project(coming, 0, 0)
                 project(coming, 0, 1)
-            if exped is not None and not last:
+            if exped is not None:
                 project(exped, 1, 1)
                 project(exped, 1, 0)
-            if k == 1:
-                table_of[0], table_pieces = rope_table(nc, const, rest)
-            for piece in table_pieces[:2]:
-                piece()
-            table_pieces = table_pieces[2:]
-            if exped is not None and (topped is not None or not last):
                 exponentiate(exped, 0)
                 exponentiate(exped, 1)
-            if topped is not None and not last:
-                subtract_top(topped)
-            if flips[1] is not None:
+            if len(flips) > 1:
                 group_words(flips[1], 0)
                 group_words(flips[1], 1)
             for n in divided:
                 finish(n)
             for i in flips:
-                if i is not None and i + LOADS < UNITS:
+                if i + LOADS < UNITS:
                     load(i + LOADS)

@@ -64,10 +64,9 @@ def zero_weights(nc, const):
 def group_weights(nc, const, raw):
     grouped = const.tile([P, 2, 2, HD, 4], BF16, align_bytes=64)
     for a in range(2):
-        nc.gpsimd.tensor_scalar(
+        nc.vector.tensor_copy(
             out=grouped[:, :, 1 - a],
-            in0=raw[:, :, :, a * HD : (a + 1) * HD].rearrange("q t m f -> q m f t"),
-            scalar1=1.0, scalar2=0.0, op0=ALU.mult, op1=ALU.add,
+            in_=raw[:, :, :, a * HD : (a + 1) * HD].rearrange("q t m f -> q m f t"),
         )
     return grouped
 
@@ -208,10 +207,10 @@ def tile_deepseekv4attention_pa_t_kernel(tc, hidden, wkv, wgate, ape, out_0, out
 
         def spread_ape():
             for a in range(2):
-                nc.gpsimd.tensor_copy(
+                nc.scalar.copy(
                     out=ape_f32[:, 0, (1 - a) * HD : (2 - a) * HD], in_=ape_rows[:, a * HD : (a + 1) * HD]
                 )
-            nc.gpsimd.tensor_copy(out=ape_f32[:, 1], in_=ape_rows[:])
+            nc.scalar.copy(out=ape_f32[:, 1], in_=ape_rows[:])
 
         def turn_ape():
             planes = psum_words.tile([P, 2, 2 * P], F32, tag="planes")
@@ -269,7 +268,7 @@ def tile_deepseekv4attention_pa_t_kernel(tc, hidden, wkv, wgate, ape, out_0, out
             operand_of[-1] = (moved_codes, moved_scales)
 
         def project(n, m, half):
-            pool = (psum_gate, psum_kv)[m]
+            pool = psum_gate if m == 0 or n == TWOS - 1 else psum_kv
             products = pool.tile([P, COLUMNS], F32, tag=f"half_{half}")
             if half == 0:
                 passes = [(2 * n, HD)]
@@ -387,6 +386,19 @@ def tile_deepseekv4attention_pa_t_kernel(tc, hidden, wkv, wgate, ape, out_0, out
             nc.vector.reciprocal(out=inverse[:], in_=inverse_of[n][:])
             inverse_of[n] = inverse
 
+        def invert_each(n):
+            inverse = work.tile([P, 1, 2 * HD], F32)
+            nc.vector.reciprocal(out=inverse[:, 0], in_=sums_of[n][:, 0, :])
+            inverse_of[n] = inverse
+
+        def divide_each(n):
+            pooled = work.tile([P, 1, 2, HD], F32)
+            pooled_of[n] = pooled
+            nc.vector.tensor_tensor(
+                out=pooled[:].rearrange("p i w f -> p i (w f)"), in0=sums_of[n][:, 1:2, :],
+                in1=inverse_of[n][:], op=ALU.mult,
+            )
+
         def scale_values(n):
             scaled = work.tile([P, 2, HD], F32)
             nc.vector.tensor_tensor(
@@ -422,8 +434,9 @@ def tile_deepseekv4attention_pa_t_kernel(tc, hidden, wkv, wgate, ape, out_0, out
                 out=rows_of(out_0, first, count)[:, :, 0 : HD - ROPE], in_=pooled[:, :, 0 : HD - ROPE]
             )
             products = work.tile([P, size, 2, HALF, 2], F32)
+            engine = nc.vector if n == TWOS - 1 else nc.gpsimd
             for o in range(2):
-                nc.gpsimd.tensor_tensor(
+                engine.tensor_tensor(
                     out=products[:, :, o],
                     in0=pooled[:, :, HD - ROPE : HD].rearrange("p w (j i) -> p w j i", i=2),
                     in1=table[:, 2 * first : 2 * first + size, o]
@@ -434,7 +447,7 @@ def tile_deepseekv4attention_pa_t_kernel(tc, hidden, wkv, wgate, ape, out_0, out
             rotated = work.tile([P, size, ROPE], F32)
             pairs = rotated[:].rearrange("p w (j i) -> p w j i", i=2)
             for i, op in ((0, ALU.subtract), (1, ALU.add)):
-                nc.gpsimd.tensor_tensor(
+                engine.tensor_tensor(
                     out=pairs[:, :, :, i],
                     in0=products[:, :, 0, :, i],
                     in1=products[:, :, 1, :, 1 - i],
@@ -452,43 +465,37 @@ def tile_deepseekv4attention_pa_t_kernel(tc, hidden, wkv, wgate, ape, out_0, out
                 flip_words(i, half)
                 group_words(i, half)
 
-        weights = group_weights(nc, const, raw)
-        spread_ape()
         for i in range(3):
             flip_and_group(i)
-        turn_pieces[0]()
+        spread_ape()
+        flip_and_group(3)
         quantise(0)
-        turn_pieces[1]()
+        weights = group_weights(nc, const, raw)
         move_on()
         quantise_weights(nc, weights, w_codes, w_scales)
         quantise(1)
+        turn_pieces[0]()
         quantise(2)
-        flip_and_group(3)
+        turn_pieces[1]()
         turn_ape()
+        flip_and_group(4)
         project(0, 0, 0)
         project(0, 0, 1)
-        table_pieces[0]()
         land(0, 0)
         quantise(3)
         land(0, 1)
-        flip_and_group(4)
-        table_pieces[1]()
-        table_pieces[2]()
+        for piece in table_pieces:
+            piece()
         for i in range(5):
             load(i + LOADS)
 
-        for k in range(TWOS + 3):
+        for k in range(TWOS):
             landing, coming, exped, weighed = pair(k), pair(k + 1), pair(k - 1), pair(k - 2)
             flips = [i for i in (2 * k + 5, 2 * k + 6) if i < UNITS]
             quantised = [i for i in (2 * k + 4, 2 * k + 5) if i < UNITS]
             summed, divided = pair(k - 3), pair(k - 4)
             summed = [] if summed is None else [summed]
             divided = [] if divided is None else [divided]
-            if k == TWOS + 2:
-                divided = [k - 4, k - 3]
-                summed = []
-            if k == TWOS + 1:
-                summed = [k - 3, k - 2]
 
             for n in divided:
                 keep_weights(n)
@@ -501,13 +508,11 @@ def tile_deepseekv4attention_pa_t_kernel(tc, hidden, wkv, wgate, ape, out_0, out
                 subtract_top(exped)
             for n in divided:
                 invert(n)
-            if landing == 0:
-                top_of_4(landing)
             if quantised:
                 quantise(quantised[0])
             for n in divided:
                 scale_values(n)
-            if landing is not None and landing > 0:
+            if landing is not None:
                 top_of_4(landing)
             for n in divided:
                 divide(n)
@@ -551,3 +556,41 @@ def tile_deepseekv4attention_pa_t_kernel(tc, hidden, wkv, wgate, ape, out_0, out
             for i in flips:
                 if i + LOADS < UNITS:
                     load(i + LOADS)
+
+        last = TWOS - 1
+        keep_weights(last - 3)
+        add_slots(last - 2, 0)
+        add_slots(last - 2, 1)
+        project(last, 1, 1)
+        project(last, 1, 0)
+        multiply_weights(last - 3)
+        subtract_top(last)
+        exponentiate(last, 1)
+        exponentiate(last, 0)
+        keep_weights(last - 2)
+        weigh(last - 1, 1)
+        weigh(last - 1, 0)
+        invert(last - 3)
+        add_slots(last - 1, 0)
+        add_slots(last - 1, 1)
+        add_slots(last, 0)
+        keep_weights(last - 1)
+        scale_values(last - 3)
+        multiply_weights(last - 2)
+        weigh(last, 1)
+        weigh(last, 0)
+        divide(last - 3)
+        finish(last - 3)
+        invert(last - 2)
+        add_slots(last, 1)
+        multiply_weights(last - 1)
+        scale_values(last - 2)
+        invert(last - 1)
+        divide(last - 2)
+        finish(last - 2)
+        scale_values(last - 1)
+        invert_each(last)
+        divide(last - 1)
+        finish(last - 1)
+        divide_each(last)
+        finish(last)

@@ -362,7 +362,7 @@ def tile_deepseekv4attention_pa_t_kernel(tc, hidden, wkv, wgate, ape, out_0, out
             for s in range(SLOTS):
                 nc.tensor.matmul(
                     out=sums_of[n][:, which, :], lhsT=tile[:, s, :], rhs=identity[:],
-                    is_transpose=True, start=(s == 0), stop=(s == SLOTS - 1),
+                    is_transpose=(which == 1 or s >= 2), start=(s == 0), stop=(s == SLOTS - 1),
                 )
 
         batches = [(n, 2) for n in range(0, TWOS - 2, 2)] + [(TWOS - 2, 1), (TWOS - 1, 1)]

@@ -25,6 +25,7 @@ THETA = 10000.0
 LOADS = 8
 UNITS = BATCH * SEQ // RATIO // P
 TWOS = UNITS // 2
+ADDED_PAIRS = TWOS - 6
 ROWS_PER_SEQ = P // BATCH
 WORDS = HID // 2
 SLOTS = 2 * RATIO
@@ -160,7 +161,8 @@ def tile_deepseekv4attention_pa_t_kernel(tc, hidden, wkv, wgate, ape, out_0, out
         order = [UNITS - 1] + list(range(UNITS - 1))
         loaded, grouped_of, operand_of, products_of = {}, {}, {}, {}
         gates_of, values_of, top_of, sums_of, inverse_of = {}, {}, {}, {}, {}
-        pooled_of, swapped_of, scaled_of = {}, {}, {}
+        pooled_of, swapped_of, scaled_of, totals_of, both_of, whole_of = {}, {}, {}, {}, {}, {}
+        half_sums_of = {}
 
         def load(i):
             j = order[i]
@@ -351,71 +353,109 @@ def tile_deepseekv4attention_pa_t_kernel(tc, hidden, wkv, wgate, ape, out_0, out
                 op=ALU.mult,
             )
 
-        def add_slots(n, which):
-            if which == 0 and n < TWOS - 5:
-                sums = psum_sums.tile([P, 2, P], F32)
-                sums_of[n] = sums
-            elif which == 0:
-                planes = psum_words.tile([P, 2, 2 * P], F32, tag="planes")
-                sums_of[n] = planes[:, :, 0:P]
-            tile = (gates_of, values_of)[which][n]
-            for s in range(SLOTS):
-                nc.tensor.matmul(
-                    out=sums_of[n][:, which, :], lhsT=tile[:, s, :], rhs=identity[:],
-                    is_transpose=(which == 1 or s >= 2), start=(s == 0), stop=(s == SLOTS - 1),
-                )
-
         batches = [(n, 2) for n in range(0, TWOS - 2, 2)] + [(TWOS - 2, 1), (TWOS - 1, 1)]
         batch_of = {n: (first, count) for first, count in batches for n in range(first, first + count)}
 
-        def keep_weights(n):
-            swapped = work.tile([P, 2, HD], F32)
-            for w in range(2):
-                nc.scalar.copy(out=swapped[:, 1 - w], in_=sums_of[n][:, 0, w * HD : (w + 1) * HD])
-            swapped_of[n] = swapped
+        def add_slots(n, which):
+            first_pair, count = batch_of[n]
+            if first_pair not in sums_of:
+                if count == 2:
+                    sums = psum_sums.tile([P, 2, 2, P], F32)
+                    sums_of[n] = sums
+                else:
+                    planes = psum_words.tile([P, 2, 2 * P], F32, tag="planes")
+                    sums_of[n] = planes[:].rearrange("p h (w c) -> p h w c", w=2)
+            out = sums_of[first_pair][:, n - first_pair, which, :]
+            if which == 0:
+                tile, count = (half_sums_of[n], RATIO) if n in half_sums_of else (gates_of[n], SLOTS)
+                parts = [tile[:, s] for s in range(count)]
+            else:
+                parts = [values_of[n][:, s] for s in range(SLOTS)]
+            for s, part in enumerate(parts):
+                nc.tensor.matmul(
+                    out=out, lhsT=part, rhs=identity[:], is_transpose=(which == 1 or s >= 2),
+                    start=(s == 0), stop=(s == len(parts) - 1),
+                )
 
-        def multiply_weights(n):
-            both = work.tile([P, 1, HD], F32)
+        def add_halves(n):
+            if n >= ADDED_PAIRS:
+                return
+            g = gates_of[n]
+            sums_4 = work.tile([P, RATIO, P], F32)
             nc.vector.tensor_tensor(
-                out=both[:, 0], in0=swapped_of[n][:, 0], in1=swapped_of[n][:, 1], op=ALU.mult
+                out=sums_4[:], in0=half_of(g, 0), in1=half_of(g, 1), op=ALU.add
             )
-            inverse_of[n] = both
+            half_sums_of[n] = sums_4
 
-        def invert(n):
+        def keep_sums(first_pair):
+            count = batch_of[first_pair][1]
+            sums = sums_of[first_pair]
+            swapped = work.tile([P, count, 2, HD], F32)
+            for w in range(2):
+                nc.scalar.copy(
+                    out=swapped[:, :, 1 - w], in_=sums[:, 0:count, 0, w * HD : (w + 1) * HD]
+                )
+            totals = work.tile([P, count, 2, HD], F32)
+            nc.scalar.copy(
+                out=totals[:].rearrange("p i w f -> p i (w f)"), in_=sums[:, 0:count, 1, :]
+            )
+            swapped_of[first_pair], totals_of[first_pair] = swapped, totals
+
+        def multiply_windows(first_pair):
+            swapped = swapped_of[first_pair]
+            both = work.tile([P, batch_of[first_pair][1], HD], F32)
+            nc.vector.tensor_tensor(
+                out=both[:], in0=swapped[:, :, 0], in1=swapped[:, :, 1], op=ALU.mult
+            )
+            both_of[first_pair] = both
+
+        def multiply_pairs(first_pair):
+            both = both_of[first_pair]
+            whole = work.tile([P, 1, HD], F32)
+            nc.vector.tensor_tensor(out=whole[:, 0], in0=both[:, 0], in1=both[:, 1], op=ALU.mult)
+            whole_of[first_pair] = whole
+
+        def invert(first_pair):
+            whole = (whole_of if batch_of[first_pair][1] == 2 else both_of)[first_pair]
             inverse = work.tile([P, 1, HD], F32)
-            nc.vector.reciprocal(out=inverse[:], in_=inverse_of[n][:])
-            inverse_of[n] = inverse
+            nc.vector.reciprocal(out=inverse[:], in_=whole[:])
+            inverse_of[first_pair] = inverse
+
+        def share_inverse(first_pair):
+            shared = work.tile([P, 2, HD], F32)
+            nc.vector.tensor_tensor(
+                out=shared[:], in0=both_of[first_pair][:, ::-1],
+                in1=inverse_of[first_pair][:].to_broadcast([P, 2, HD]), op=ALU.mult,
+            )
+            inverse_of[first_pair] = shared
+
+        def scale_values(first_pair):
+            count = batch_of[first_pair][1]
+            scaled = work.tile([P, count, 2, HD], F32)
+            nc.vector.tensor_tensor(
+                out=scaled[:], in0=totals_of[first_pair][:],
+                in1=inverse_of[first_pair][:].unsqueeze(2).to_broadcast([P, count, 2, HD]), op=ALU.mult,
+            )
+            scaled_of[first_pair] = scaled
+
+        def divide(first_pair):
+            pooled = work.tile([P, batch_of[first_pair][1], 2, HD], F32)
+            nc.vector.tensor_tensor(
+                out=pooled[:], in0=scaled_of[first_pair][:], in1=swapped_of[first_pair][:], op=ALU.mult
+            )
+            pooled_of[first_pair] = pooled
 
         def invert_each(n):
-            inverse = work.tile([P, 1, 2 * HD], F32)
-            nc.vector.reciprocal(out=inverse[:, 0], in_=sums_of[n][:, 0, :])
+            inverse = work.tile([P, 2 * HD], F32, tag="inverse_each")
+            nc.vector.reciprocal(out=inverse[:], in_=sums_of[n][:, 0, 0, :])
             inverse_of[n] = inverse
 
         def divide_each(n):
             pooled = work.tile([P, 1, 2, HD], F32)
             pooled_of[n] = pooled
             nc.vector.tensor_tensor(
-                out=pooled[:].rearrange("p i w f -> p i (w f)"), in0=sums_of[n][:, 1:2, :],
+                out=pooled[:].rearrange("p i w f -> p (i w f)"), in0=sums_of[n][:, 0, 1, :],
                 in1=inverse_of[n][:], op=ALU.mult,
-            )
-
-        def scale_values(n):
-            scaled = work.tile([P, 2, HD], F32)
-            nc.vector.tensor_tensor(
-                out=scaled[:],
-                in0=sums_of[n][:, 1, :].rearrange("p (w f) -> p w f", w=2),
-                in1=inverse_of[n][:].to_broadcast([P, 2, HD]),
-                op=ALU.mult,
-            )
-            scaled_of[n] = scaled
-
-        def divide(n):
-            first, count = batch_of[n]
-            if n == first:
-                pooled = work.tile([P, count, 2, HD], F32)
-                pooled_of[first] = pooled
-            nc.vector.tensor_tensor(
-                out=pooled_of[first][:, n - first], in0=scaled_of[n][:], in1=swapped_of[n][:], op=ALU.mult
             )
 
         def rows_of(out, first, count):
@@ -423,10 +463,8 @@ def tile_deepseekv4attention_pa_t_kernel(tc, hidden, wkv, wgate, ape, out_0, out
                 :, 2 * first : 2 * (first + count), :
             ]
 
-        def finish(n):
-            first, count = batch_of[n]
-            if n != first + count - 1:
-                return
+        def finish(first):
+            count = batch_of[first][1]
             size = 2 * count
             pooled = pooled_of[first][:].rearrange("p i w f -> p (i w) f")
             nc.sync.dma_start(out=rows_of(out_1, first, count), in_=pooled)
@@ -434,7 +472,7 @@ def tile_deepseekv4attention_pa_t_kernel(tc, hidden, wkv, wgate, ape, out_0, out
                 out=rows_of(out_0, first, count)[:, :, 0 : HD - ROPE], in_=pooled[:, :, 0 : HD - ROPE]
             )
             products = work.tile([P, size, 2, HALF, 2], F32)
-            engine = nc.vector if n == TWOS - 1 else nc.gpsimd
+            engine = nc.vector if first == TWOS - 1 else nc.gpsimd
             for o in range(2):
                 engine.tensor_tensor(
                     out=products[:, :, o],
@@ -493,37 +531,39 @@ def tile_deepseekv4attention_pa_t_kernel(tc, hidden, wkv, wgate, ape, out_0, out
             landing, coming, exped, weighed = pair(k), pair(k + 1), pair(k - 1), pair(k - 2)
             flips = [i for i in (2 * k + 5, 2 * k + 6) if i < UNITS]
             quantised = [i for i in (2 * k + 4, 2 * k + 5) if i < UNITS]
-            summed, divided = pair(k - 3), pair(k - 4)
-            summed = [] if summed is None else [summed]
-            divided = [] if divided is None else [divided]
+            summed = pair(k - 3)
+            divided = pair(k - 5) if k % 2 == 1 else None
+            finished = pair(k - 6) if k % 2 == 0 else None
 
-            for n in divided:
-                keep_weights(n)
-            if landing is not None and landing > 0:
+            if divided is not None:
+                keep_sums(divided)
+            if landing > 0:
                 land(landing, 0)
                 land(landing, 1)
-            for n in divided:
-                multiply_weights(n)
+            if divided is not None:
+                multiply_windows(divided)
             if exped is not None:
                 subtract_top(exped)
-            for n in divided:
-                invert(n)
+            if divided is not None:
+                multiply_pairs(divided)
+            if finished is not None:
+                scale_values(finished)
             if quantised:
                 quantise(quantised[0])
-            for n in divided:
-                scale_values(n)
-            if landing is not None:
-                top_of_4(landing)
-            for n in divided:
-                divide(n)
+            if divided is not None:
+                invert(divided)
+            top_of_4(landing)
+            if divided is not None:
+                share_inverse(divided)
+            if finished is not None:
+                divide(finished)
             if weighed is not None:
                 weigh(weighed, 1)
-            if landing is not None:
-                top_of_2(landing)
+                add_halves(weighed)
+            top_of_2(landing)
             if weighed is not None:
                 weigh(weighed, 0)
-            if landing is not None:
-                top_of_1(landing)
+            top_of_1(landing)
             if flips:
                 flip_words(flips[0], 0)
                 flip_words(flips[0], 1)
@@ -532,14 +572,14 @@ def tile_deepseekv4attention_pa_t_kernel(tc, hidden, wkv, wgate, ape, out_0, out
             if k < 3 and coming is not None:
                 project(coming, 0, 0)
                 project(coming, 0, 1)
+            if summed is not None:
+                add_slots(summed, 1)
+                add_slots(summed, 0)
             if len(flips) > 1:
                 flip_words(flips[1], 0)
                 flip_words(flips[1], 1)
             if len(quantised) > 1:
                 quantise(quantised[1])
-            for n in summed:
-                add_slots(n, 0)
-                add_slots(n, 1)
             if k >= 3 and coming is not None:
                 project(coming, 0, 0)
                 project(coming, 0, 1)
@@ -551,46 +591,47 @@ def tile_deepseekv4attention_pa_t_kernel(tc, hidden, wkv, wgate, ape, out_0, out
             if len(flips) > 1:
                 group_words(flips[1], 0)
                 group_words(flips[1], 1)
-            for n in divided:
-                finish(n)
+            if finished is not None:
+                finish(finished)
             for i in flips:
                 if i + LOADS < UNITS:
                     load(i + LOADS)
 
         last = TWOS - 1
-        keep_weights(last - 3)
-        add_slots(last - 2, 0)
         add_slots(last - 2, 1)
+        add_slots(last - 2, 0)
         project(last, 1, 1)
         project(last, 1, 0)
-        multiply_weights(last - 3)
         subtract_top(last)
+        scale_values(last - 5)
         exponentiate(last, 1)
         exponentiate(last, 0)
-        keep_weights(last - 2)
         weigh(last - 1, 1)
+        add_halves(last - 1)
+        divide(last - 5)
         weigh(last - 1, 0)
-        invert(last - 3)
-        add_slots(last - 1, 0)
+        add_halves(last)
+        finish(last - 5)
+        keep_sums(last - 3)
         add_slots(last - 1, 1)
-        add_slots(last, 0)
-        keep_weights(last - 1)
-        scale_values(last - 3)
-        multiply_weights(last - 2)
+        add_slots(last - 1, 0)
+        multiply_windows(last - 3)
         weigh(last, 1)
+        multiply_pairs(last - 3)
         weigh(last, 0)
+        invert(last - 3)
+        keep_sums(last - 1)
+        add_slots(last, 0)
+        add_slots(last, 1)
+        multiply_windows(last - 1)
+        share_inverse(last - 3)
+        invert(last - 1)
+        scale_values(last - 3)
+        scale_values(last - 1)
         divide(last - 3)
         finish(last - 3)
-        invert(last - 2)
-        add_slots(last, 1)
-        multiply_weights(last - 1)
-        scale_values(last - 2)
-        invert(last - 1)
-        divide(last - 2)
-        finish(last - 2)
-        scale_values(last - 1)
-        invert_each(last)
         divide(last - 1)
         finish(last - 1)
+        invert_each(last)
         divide_each(last)
         finish(last)

@@ -22,10 +22,10 @@ FEAT = 2 * HD
 ROPE = 32
 HALF = ROPE // 2
 THETA = 10000.0
+WARM_UPS = 6
 LOADS = 8
 UNITS = BATCH * SEQ // RATIO // P
 TWOS = UNITS // 2
-ADDED_PAIRS = TWOS - 6
 ROWS_PER_SEQ = P // BATCH
 WORDS = HID // 2
 SLOTS = 2 * RATIO
@@ -162,7 +162,6 @@ def tile_deepseekv4attention_pa_t_kernel(tc, hidden, wkv, wgate, ape, out_0, out
         loaded, grouped_of, operand_of, products_of = {}, {}, {}, {}
         gates_of, values_of, top_of, sums_of, inverse_of = {}, {}, {}, {}, {}
         pooled_of, swapped_of, scaled_of, totals_of, both_of, whole_of = {}, {}, {}, {}, {}, {}
-        half_sums_of = {}
 
         def load(i):
             j = order[i]
@@ -198,6 +197,16 @@ def tile_deepseekv4attention_pa_t_kernel(tc, hidden, wkv, wgate, ape, out_0, out
         nc.vector.tensor_copy(out=position[:], in_=position_int[:])
         identity = const.tile([P, P], F32)
         make_identity(nc, identity[:])
+        zeros = const.tile([P, P], F32)
+        nc.vector.memset(zeros[:], 0.0)
+
+        def keep_warm(count):
+            planes = psum_words.tile([P, 2, 2 * P], F32, tag="planes")
+            for s in range(count):
+                nc.tensor.matmul(
+                    out=planes[:, 0, 0:P], lhsT=zeros[:], rhs=zeros[:], start=True, stop=True
+                )
+
         nothing = const.tile([P, 1], F32)
         nc.vector.memset(nothing[:], 0.0)
         nc.scalar.activation(out=nothing[:], in_=nothing[:], func=ACT.Sin)
@@ -366,26 +375,12 @@ def tile_deepseekv4attention_pa_t_kernel(tc, hidden, wkv, wgate, ape, out_0, out
                     planes = psum_words.tile([P, 2, 2 * P], F32, tag="planes")
                     sums_of[n] = planes[:].rearrange("p h (w c) -> p h w c", w=2)
             out = sums_of[first_pair][:, n - first_pair, which, :]
-            if which == 0:
-                tile, count = (half_sums_of[n], RATIO) if n in half_sums_of else (gates_of[n], SLOTS)
-                parts = [tile[:, s] for s in range(count)]
-            else:
-                parts = [values_of[n][:, s] for s in range(SLOTS)]
-            for s, part in enumerate(parts):
+            tile = (gates_of, values_of)[which][n]
+            for s in range(SLOTS):
                 nc.tensor.matmul(
-                    out=out, lhsT=part, rhs=identity[:], is_transpose=(which == 1 or s >= 2),
-                    start=(s == 0), stop=(s == len(parts) - 1),
+                    out=out, lhsT=tile[:, s], rhs=identity[:], is_transpose=True,
+                    start=(s == 0), stop=(s == SLOTS - 1),
                 )
-
-        def add_halves(n):
-            if n >= ADDED_PAIRS:
-                return
-            g = gates_of[n]
-            sums_4 = work.tile([P, RATIO, P], F32)
-            nc.vector.tensor_tensor(
-                out=sums_4[:], in0=half_of(g, 0), in1=half_of(g, 1), op=ALU.add
-            )
-            half_sums_of[n] = sums_4
 
         def keep_sums(first_pair):
             count = batch_of[first_pair][1]
@@ -503,6 +498,7 @@ def tile_deepseekv4attention_pa_t_kernel(tc, hidden, wkv, wgate, ape, out_0, out
                 flip_words(i, half)
                 group_words(i, half)
 
+        keep_warm(WARM_UPS)
         for i in range(3):
             flip_and_group(i)
         spread_ape()
@@ -557,35 +553,34 @@ def tile_deepseekv4attention_pa_t_kernel(tc, hidden, wkv, wgate, ape, out_0, out
                 share_inverse(divided)
             if finished is not None:
                 divide(finished)
-            if weighed is not None:
-                weigh(weighed, 1)
-                add_halves(weighed)
-            top_of_2(landing)
-            if weighed is not None:
-                weigh(weighed, 0)
-            top_of_1(landing)
             if flips:
                 flip_words(flips[0], 0)
                 flip_words(flips[0], 1)
                 group_words(flips[0], 0)
                 group_words(flips[0], 1)
-            if k < 3 and coming is not None:
+            if weighed is not None:
+                project(weighed, 1, 0)
+            if coming is not None:
                 project(coming, 0, 0)
-                project(coming, 0, 1)
             if summed is not None:
-                add_slots(summed, 1)
                 add_slots(summed, 0)
+                add_slots(summed, 1)
             if len(flips) > 1:
                 flip_words(flips[1], 0)
                 flip_words(flips[1], 1)
-            if len(quantised) > 1:
-                quantise(quantised[1])
-            if k >= 3 and coming is not None:
-                project(coming, 0, 0)
+            if coming is not None:
                 project(coming, 0, 1)
+            if weighed is not None:
+                weigh(weighed, 1)
+            top_of_2(landing)
+            if weighed is not None:
+                weigh(weighed, 0)
+            top_of_1(landing)
             if exped is not None:
                 project(exped, 1, 1)
-                project(exped, 1, 0)
+            if len(quantised) > 1:
+                quantise(quantised[1])
+            if exped is not None:
                 exponentiate(exped, 0)
                 exponentiate(exped, 1)
             if len(flips) > 1:
@@ -600,6 +595,7 @@ def tile_deepseekv4attention_pa_t_kernel(tc, hidden, wkv, wgate, ape, out_0, out
         last = TWOS - 1
         add_slots(last - 2, 1)
         add_slots(last - 2, 0)
+        project(last - 1, 1, 0)
         project(last, 1, 1)
         project(last, 1, 0)
         subtract_top(last)
@@ -607,10 +603,8 @@ def tile_deepseekv4attention_pa_t_kernel(tc, hidden, wkv, wgate, ape, out_0, out
         exponentiate(last, 1)
         exponentiate(last, 0)
         weigh(last - 1, 1)
-        add_halves(last - 1)
         divide(last - 5)
         weigh(last - 1, 0)
-        add_halves(last)
         finish(last - 5)
         keep_sums(last - 3)
         add_slots(last - 1, 1)

@@ -244,11 +244,11 @@ def tile_deepseekv4attention_pa_t_kernel(tc, hidden, wkv, wgate, ape, out_0, out
                     )
             grouped_of[(i, half)] = planes
 
-        def group_words(i, half):
+        def group_words(i, half, copy=nc.scalar.copy):
             if half == 0:
                 grouped = words.tile([P, COLUMNS, 4], BF16, align_bytes=64)
                 grouped_of[i] = grouped
-            nc.scalar.copy(
+            copy(
                 out=grouped_of[i][:].bitcast(F32)[:, 2 * half * P : 2 * (half + 1) * P, :],
                 in_=grouped_of[(i, half)][:].rearrange("q u c -> q c u"),
             )
@@ -424,10 +424,10 @@ def tile_deepseekv4attention_pa_t_kernel(tc, hidden, wkv, wgate, ape, out_0, out
             )
             inverse_of[first_pair] = shared
 
-        def scale_values(first_pair):
+        def scale_values(first_pair, engine=nc.vector):
             count = batch_of[first_pair][1]
             scaled = work.tile([P, count, 2, HD], F32)
-            nc.vector.tensor_tensor(
+            engine.tensor_tensor(
                 out=scaled[:], in0=totals_of[first_pair][:],
                 in1=inverse_of[first_pair][:].unsqueeze(2).to_broadcast([P, count, 2, HD]), op=ALU.mult,
             )
@@ -499,27 +499,36 @@ def tile_deepseekv4attention_pa_t_kernel(tc, hidden, wkv, wgate, ape, out_0, out
                 group_words(i, half)
 
         keep_warm(WARM_UPS)
-        for i in range(3):
-            flip_and_group(i)
-        spread_ape()
-        flip_and_group(3)
+        turn_pieces[0]()
+        flip_and_group(0)
+        turn_pieces[1]()
         quantise(0)
+        flip_and_group(1)
+        flip_and_group(2)
+        spread_ape()
+        table_pieces[0]()
+        flip_words(3, 0)
+        group_words(3, 0)
+        flip_words(3, 1)
+        table_pieces[1]()
+        table_pieces[2]()
         weights = group_weights(nc, const, raw)
         move_on()
         quantise_weights(nc, weights, w_codes, w_scales)
         quantise(1)
-        turn_pieces[0]()
         quantise(2)
-        turn_pieces[1]()
+        group_words(3, 1, nc.vector.tensor_copy)
         turn_ape()
-        flip_and_group(4)
+        flip_words(4, 0)
+        group_words(4, 0)
+        flip_words(4, 1)
         project(0, 0, 0)
         project(0, 0, 1)
-        land(0, 0)
         quantise(3)
+        land(0, 0)
+        group_words(4, 1, nc.vector.tensor_copy)
         land(0, 1)
-        for piece in table_pieces:
-            piece()
+        nc.scalar.activation(out=nothing[:], in_=nothing[:], func=ACT.Exp)
         for i in range(5):
             load(i + LOADS)
 
@@ -536,28 +545,28 @@ def tile_deepseekv4attention_pa_t_kernel(tc, hidden, wkv, wgate, ape, out_0, out
             if landing > 0:
                 land(landing, 0)
                 land(landing, 1)
-            if divided is not None:
-                multiply_windows(divided)
             if exped is not None:
                 subtract_top(exped)
             if divided is not None:
-                multiply_pairs(divided)
-            if finished is not None:
-                scale_values(finished)
+                multiply_windows(divided)
             if quantised:
                 quantise(quantised[0])
+            if divided is not None:
+                multiply_pairs(divided)
             if divided is not None:
                 invert(divided)
             top_of_4(landing)
             if divided is not None:
                 share_inverse(divided)
+                scale_values(divided, nc.gpsimd)
             if finished is not None:
                 divide(finished)
             if flips:
                 flip_words(flips[0], 0)
                 flip_words(flips[0], 1)
                 group_words(flips[0], 0)
-                group_words(flips[0], 1)
+                if k >= 2:
+                    group_words(flips[0], 1)
             if weighed is not None:
                 project(weighed, 1, 0)
             if coming is not None:
@@ -578,6 +587,8 @@ def tile_deepseekv4attention_pa_t_kernel(tc, hidden, wkv, wgate, ape, out_0, out
             top_of_1(landing)
             if exped is not None:
                 project(exped, 1, 1)
+            if k < 2:
+                group_words(flips[0], 1, nc.vector.tensor_copy)
             if len(quantised) > 1:
                 quantise(quantised[1])
             if exped is not None:
@@ -593,22 +604,21 @@ def tile_deepseekv4attention_pa_t_kernel(tc, hidden, wkv, wgate, ape, out_0, out
                     load(i + LOADS)
 
         last = TWOS - 1
-        add_slots(last - 2, 1)
         add_slots(last - 2, 0)
+        add_slots(last - 2, 1)
         project(last - 1, 1, 0)
         project(last, 1, 1)
         project(last, 1, 0)
         subtract_top(last)
-        scale_values(last - 5)
         exponentiate(last, 1)
         exponentiate(last, 0)
         weigh(last - 1, 1)
         divide(last - 5)
-        weigh(last - 1, 0)
         finish(last - 5)
+        weigh(last - 1, 0)
         keep_sums(last - 3)
-        add_slots(last - 1, 1)
         add_slots(last - 1, 0)
+        add_slots(last - 1, 1)
         multiply_windows(last - 3)
         weigh(last, 1)
         multiply_pairs(last - 3)
@@ -617,15 +627,15 @@ def tile_deepseekv4attention_pa_t_kernel(tc, hidden, wkv, wgate, ape, out_0, out
         keep_sums(last - 1)
         add_slots(last, 0)
         add_slots(last, 1)
-        multiply_windows(last - 1)
         share_inverse(last - 3)
-        invert(last - 1)
+        multiply_windows(last - 1)
         scale_values(last - 3)
-        scale_values(last - 1)
+        invert(last - 1)
         divide(last - 3)
         finish(last - 3)
+        scale_values(last - 1)
+        invert_each(last)
         divide(last - 1)
         finish(last - 1)
-        invert_each(last)
         divide_each(last)
         finish(last)

from contextlib import ExitStack
import math

import concourse.mybir as mybir
from concourse.masks import make_identity

F32 = mybir.dt.float32
BF16 = mybir.dt.bfloat16
I32 = mybir.dt.int32
U32 = mybir.dt.uint32
U8 = mybir.dt.uint8
FP8X4 = mybir.dt.float8_e4m3fn_x4
ALU = mybir.AluOpType
ACT = mybir.ActivationFunctionType
ENGINES = mybir.EngineType

P = 128
BATCH, SEQ, HID = 4, 4096, 512
RATIO = 4
HD = 64
FEAT = 2 * HD
ROPE = 32
HALF = ROPE // 2
THETA = 10000.0
WARM_UPS = 6
LOADS = 8
UNITS = BATCH * SEQ // RATIO // P
TWOS = UNITS // 2
ROWS_PER_SEQ = P // BATCH
WORDS = HID // 2
SLOTS = 2 * RATIO
COLUMNS = RATIO * P
MINUS_BIG = -1.0e30
ROUND_MAGIC = 1.5 * 2.0**23

FLOPS = 2 * BATCH * SEQ * HID * 2 * FEAT


def leading_bits(x, bits):
    if x == 0.0:
        return 0.0
    step = 1.0
    while abs(x) / step >= 2.0**bits:
        step *= 2.0
    while abs(x) / step < 2.0 ** (bits - 1):
        step /= 2.0
    return round(x / step) * step


def load_weights(nc, const, wgate, wkv):
    raw = const.tile([P, 4, 2, FEAT], BF16)
    for m, w in enumerate((wgate, wkv)):
        nc.sync.dma_start(out=raw[:, :, m, :], in_=w.rearrange("(q t) c -> q t c", t=4))
    return raw


def zero_weights(nc, const):
    w_codes = const.tile([P, 2, 4 * HD], U32, align_bytes=64)
    w_scales = const.tile([P, 2, 4 * HD], U8, align_bytes=64)
    nc.gpsimd.memset(w_codes[:], 0)
    nc.gpsimd.memset(w_scales[:], 0)
    return w_codes, w_scales


def group_weights(nc, const, raw):
    grouped = const.tile([P, 2, 2, HD, 4], BF16, align_bytes=64)
    for a in range(2):
        nc.vector.tensor_copy(
            out=grouped[:, :, 1 - a],
            in_=raw[:, :, :, a * HD : (a + 1) * HD].rearrange("q t m f -> q m f t"),
        )
    return grouped


def quantise_weights(nc, grouped, w_codes, w_scales):
    for m in range(2):
        nc.vector.quantize_mx(
            out=w_codes[:, m, HD : 3 * HD].bitcast(FP8X4),
            scales=w_scales[:, m, HD : 3 * HD],
            in_=grouped[:, m].rearrange("q a f t -> q (a f t)"),
        )


def number_positions(nc, const):
    position_int = const.tile([P, UNITS], I32)
    for b in range(BATCH):
        nc.gpsimd.iota(
            position_int[b * ROWS_PER_SEQ : (b + 1) * ROWS_PER_SEQ, :],
            pattern=[[RATIO, UNITS]], base=0, channel_multiplier=RATIO * UNITS,
        )
    return position_int


def rope_turns(nc, const, position):
    nearest = const.tile([P, HALF, UNITS], F32)
    turns_hi = const.tile([P, HALF, UNITS], F32)
    turns_lo = const.tile([P, HALF, UNITS], F32)
    for i in range(HALF):
        frequency = 1.0 / THETA ** (i / HALF) / (2.0 * math.pi)
        leading = leading_bits(frequency, 12)
        nc.vector.tensor_scalar(
            out=nearest[:, i], in0=position[:], scalar1=frequency, scalar2=ROUND_MAGIC,
            op0=ALU.mult, op1=ALU.add,
        )
        nc.vector.tensor_scalar(
            out=turns_hi[:, i], in0=position[:], scalar1=leading, scalar2=None, op0=ALU.mult
        )
        nc.scalar.activation(
            out=turns_lo[:, i], in_=position[:], func=ACT.Copy, scale=frequency - leading
        )
    minus_rest = const.tile([P, HALF, UNITS], F32)
    rest = const.tile([P, HALF, UNITS], F32)
    pieces = [
        lambda: nc.vector.scalar_tensor_tensor(
            out=minus_rest[:], in0=nearest[:], scalar=ROUND_MAGIC, in1=turns_hi[:],
            op0=ALU.subtract, op1=ALU.subtract,
        ),
        lambda: nc.vector.tensor_tensor(
            out=rest[:], in0=turns_lo[:], in1=minus_rest[:], op=ALU.subtract
        ),
    ]
    return rest, pieces


def rope_table(nc, const, rest):
    size = const.tile([P, HALF, UNITS], F32)
    table = const.tile([P, UNITS, 2, HALF], F32)
    turn = 2.0 * math.pi
    activation = nc.scalar.activation
    pieces = [
        lambda: activation(
            out=table[:, :, 1], in_=rest[:].rearrange("p i j -> p j i"), func=ACT.Sin, scale=turn
        ),
        lambda: activation(out=size[:], in_=rest[:], func=ACT.Abs),
        lambda: activation(
            out=table[:, :, 0], in_=size[:].rearrange("p i j -> p j i"), func=ACT.Sin, scale=-turn,
            bias=math.pi / 2.0,
        ),
    ]
    return table, pieces


def tile_deepseekv4attention_pa_t_kernel(tc, hidden, wkv, wgate, ape, out_0, out_1):
    nc = tc.nc
    with ExitStack() as ctx:
        const = ctx.enter_context(tc.tile_pool(name="const", bufs=1))
        first = ctx.enter_context(tc.tile_pool(name="first", bufs=2))
        tokens = ctx.enter_context(tc.tile_pool(name="tokens", bufs=LOADS))
        words = ctx.enter_context(tc.tile_pool(name="words", bufs=6))
        operand = ctx.enter_context(tc.tile_pool(name="operand", bufs=12))
        gates_pool = ctx.enter_context(tc.tile_pool(name="gates_pool", bufs=6))
        values_pool = ctx.enter_context(tc.tile_pool(name="values_pool", bufs=5))
        work = ctx.enter_context(tc.tile_pool(name="work", bufs=3))
        psum_words = ctx.enter_context(tc.psum_pool(name="psum_words", bufs=3))
        psum_gate = ctx.enter_context(tc.psum_pool(name="psum_gate", bufs=1))
        psum_kv = ctx.enter_context(tc.psum_pool(name="psum_kv", bufs=1))
        psum_sums = ctx.enter_context(tc.psum_pool(name="psum_sums", bufs=1))

        tokens_of_row = hidden.rearrange("b s k -> (b s) k").rearrange("(p t) k -> p (t k)", p=P)

        order = [UNITS - 1] + list(range(UNITS - 1))
        loaded, grouped_of, operand_of, products_of = {}, {}, {}, {}
        gates_of, values_of, top_of, sums_of, inverse_of = {}, {}, {}, {}, {}
        pooled_of, swapped_of, scaled_of, totals_of, both_of, whole_of = {}, {}, {}, {}, {}, {}

        def load(i):
            j = order[i]
            pieces = 2 if i == 0 else 1
            width = RATIO * HID // pieces
            loaded[i] = []
            for h in range(pieces):
                if i == 0:
                    x = first.tile([P, width], BF16)
                else:
                    x = tokens.tile([P, width], BF16)
                begin = j * RATIO * HID + h * width
                nc.sync.dma_start(out=x[:], in_=tokens_of_row[:, begin : begin + width])
                loaded[i] += [(x, r * HID) for r in range(RATIO // pieces)]

        load(0)
        load(1)
        raw = load_weights(nc, const, wgate, wkv)
        load(2)
        position_int = number_positions(nc, const)
        ape_rows = const.tile([P, FEAT], BF16)
        nc.gpsimd.memset(ape_rows[:], 0.0)
        nc.sync.dma_start(out=ape_rows[0:RATIO, :], in_=ape)
        for i in range(3, LOADS):
            load(i)

        ctx.enter_context(
            tc.manual_schedule(
                engines={ENGINES.PE, ENGINES.Activation, ENGINES.DVE, ENGINES.Pool}
            )
        )
        position = const.tile([P, UNITS], F32)
        nc.vector.tensor_copy(out=position[:], in_=position_int[:])
        identity = const.tile([P, P], F32)
        make_identity(nc, identity[:])
        zeros = const.tile([P, P], F32)
        nc.vector.memset(zeros[:], 0.0)

        def keep_warm(count):
            planes = psum_words.tile([P, 2, 2 * P], F32, tag="planes")
            for s in range(count):
                nc.tensor.matmul(
                    out=planes[:, 0, 0:P], lhsT=zeros[:], rhs=zeros[:], start=True, stop=True
                )

        nothing = const.tile([P, 1], F32)
        nc.vector.memset(nothing[:], 0.0)
        nc.scalar.activation(out=nothing[:], in_=nothing[:], func=ACT.Sin)
        w_codes, w_scales = zero_weights(nc, const)
        rest, turn_pieces = rope_turns(nc, const, position)
        table, table_pieces = rope_table(nc, const, rest)
        ape_f32 = const.tile([P, 2, FEAT], F32)
        ape_columns = const.tile([P, SLOTS], F32)

        def spread_ape():
            for a in range(2):
                nc.scalar.copy(
                    out=ape_f32[:, 0, (1 - a) * HD : (2 - a) * HD], in_=ape_rows[:, a * HD : (a + 1) * HD]
                )
            nc.scalar.copy(out=ape_f32[:, 1], in_=ape_rows[:])

        def turn_ape():
            planes = psum_words.tile([P, 2, 2 * P], F32, tag="planes")
            for half in range(2):
                nc.tensor.transpose(planes[:, half, 0:P], ape_f32[:, half], identity[:])
            nc.scalar.copy(
                out=ape_columns[:].rearrange("p (h r) -> p h r", h=2), in_=planes[:, :, 0:RATIO]
            )

        def flip_words(i, half):
            planes = psum_words.tile([P, 2, 2 * P], F32, tag="planes")
            for r in (2 * half, 2 * half + 1):
                x, begin = loaded[i][r]
                x_words = x[:, begin : begin + HID].bitcast(F32)
                for u in range(2):
                    nc.tensor.transpose(
                        planes[:, u, (r % 2) * P : (r % 2 + 1) * P],
                        x_words[:, u : WORDS : 2],
                        identity[:],
                    )
            grouped_of[(i, half)] = planes

        def group_words(i, half, copy=nc.scalar.copy):
            if half == 0:
                grouped = words.tile([P, COLUMNS, 4], BF16, align_bytes=64)
                grouped_of[i] = grouped
            copy(
                out=grouped_of[i][:].bitcast(F32)[:, 2 * half * P : 2 * (half + 1) * P, :],
                in_=grouped_of[(i, half)][:].rearrange("q u c -> q c u"),
            )

        def quantise(i):
            pool = const if i == 0 else operand
            codes = pool.tile([P, COLUMNS], U32, align_bytes=64)
            scales = pool.tile([P, COLUMNS], U8, align_bytes=64)
            nc.vector.quantize_mx(
                out=codes[:].bitcast(FP8X4),
                scales=scales[:],
                in_=grouped_of[i][:].rearrange("q c t -> q (c t)"),
            )
            operand_of[order[i]] = (codes, scales)

        def move_on():
            codes, scales = operand_of[UNITS - 1]
            moved_codes = const.tile([P, COLUMNS], U32, align_bytes=64)
            moved_scales = const.tile([P, COLUMNS], U8, align_bytes=64)
            moves = ((moved_codes, codes, I32), (moved_scales, scales, U8))
            for to_columns, of_columns in (((1, P), (0, P - 1)), ((0, 1), (P - 1, P))):
                for moved, source, dtype in moves:
                    to = moved[:].bitcast(dtype).rearrange("q (r c) -> q r c", c=P)
                    of = source[:].bitcast(dtype).rearrange("q (r c) -> q r c", c=P)
                    nc.vector.tensor_copy(
                        out=to[:, :, slice(*to_columns)], in_=of[:, :, slice(*of_columns)]
                    )
            operand_of[-1] = (moved_codes, moved_scales)

        def project(n, m, half):
            pool = psum_gate if m == 0 or n == TWOS - 1 else psum_kv
            products = pool.tile([P, COLUMNS], F32, tag=f"half_{half}")
            if half == 0:
                passes = [(2 * n, HD)]
            else:
                passes = [(2 * n - 1, 2 * HD), (2 * n + 1, 0)]
            for unit, first in passes:
                codes, scales = operand_of[unit]
                nc.tensor.matmul_mx(
                    out=products[:],
                    lhsT=w_codes[:, m, first : first + P].bitcast(FP8X4),
                    lhsT_scale=w_scales[:, m, first : first + P],
                    rhs=codes[:].bitcast(FP8X4),
                    rhs_scale=scales[:],
                    start=(unit == passes[0][0]),
                    stop=(unit == passes[-1][0]),
                )
            products_of[(n, m, half)] = products

        def half_of(tile, half):
            return tile[:, half * RATIO : (half + 1) * RATIO, :]

        def land(n, half):
            if n not in gates_of:
                gates = gates_pool.tile([P, SLOTS, P], F32)
                gates_of[n] = gates
            if n == 0:
                nc.vector.tensor_tensor(
                    out=half_of(gates_of[n], half),
                    in0=products_of[(n, 0, half)][:].rearrange("f (r p) -> f r p", r=RATIO),
                    in1=ape_columns[:, half * RATIO : (half + 1) * RATIO].unsqueeze(2).to_broadcast([P, RATIO, P]),
                    op=ALU.add,
                )
            for r in range(RATIO if n > 0 else 0):
                slot = half * RATIO + r
                nc.scalar.activation(
                    out=gates_of[n][:, slot, :],
                    in_=products_of[(n, 0, half)][:, r * P : (r + 1) * P],
                    func=ACT.Identity,
                    bias=ape_columns[:, slot : slot + 1],
                )
            if n == 0 and half == 1:
                nc.vector.memset(gates_of[n][0:HD, RATIO:SLOTS, 0:P:ROWS_PER_SEQ], MINUS_BIG)

        def top_of_4(n):
            g = gates_of[n]
            top_4 = work.tile([P, 4, P], F32)
            nc.vector.tensor_tensor(out=top_4[:], in0=g[:, 0:4], in1=g[:, 4:8], op=ALU.max)
            top_of[n] = top_4

        def top_of_2(n):
            top_4 = top_of[n]
            top_2 = work.tile([P, 2, P], F32)
            nc.vector.tensor_tensor(out=top_2[:], in0=top_4[:, 0:2], in1=top_4[:, 2:4], op=ALU.max)
            top_of[n] = top_2

        def top_of_1(n):
            top_2 = top_of[n]
            top = work.tile([P, 1, P], F32)
            nc.vector.tensor_tensor(out=top[:, 0], in0=top_2[:, 0], in1=top_2[:, 1], op=ALU.max)
            top_of[n] = top

        def subtract_top(n):
            g = gates_of[n]
            nc.vector.tensor_tensor(
                out=g[:], in0=g[:], in1=top_of[n][:].to_broadcast([P, SLOTS, P]), op=ALU.subtract
            )

        def exponentiate(n, half):
            g = half_of(gates_of[n], half)
            nc.scalar.activation(out=g, in_=g, func=ACT.Exp)

        def weigh(n, half):
            if n not in values_of:
                values = values_pool.tile([P, SLOTS, P], F32)
                values_of[n] = values
            nc.vector.tensor_tensor(
                out=half_of(values_of[n], half),
                in0=products_of[(n, 1, half)][:].rearrange("f (r p) -> f r p", r=RATIO),
                in1=half_of(gates_of[n], half),
                op=ALU.mult,
            )

        batches = [(n, 2) for n in range(0, TWOS - 2, 2)] + [(TWOS - 2, 1), (TWOS - 1, 1)]
        batch_of = {n: (first, count) for first, count in batches for n in range(first, first + count)}

        def add_slots(n, which):
            first_pair, count = batch_of[n]
            if first_pair not in sums_of:
                if count == 2:
                    sums = psum_sums.tile([P, 2, 2, P], F32)
                    sums_of[n] = sums
                else:
                    planes = psum_words.tile([P, 2, 2 * P], F32, tag="planes")
                    sums_of[n] = planes[:].rearrange("p h (w c) -> p h w c", w=2)
            out = sums_of[first_pair][:, n - first_pair, which, :]
            tile = (gates_of, values_of)[which][n]
            for s in range(SLOTS):
                nc.tensor.matmul(
                    out=out, lhsT=tile[:, s], rhs=identity[:], is_transpose=True,
                    start=(s == 0), stop=(s == SLOTS - 1),
                )

        def keep_sums(first_pair):
            count = batch_of[first_pair][1]
            sums = sums_of[first_pair]
            swapped = work.tile([P, count, 2, HD], F32)
            for w in range(2):
                nc.scalar.copy(
                    out=swapped[:, :, 1 - w], in_=sums[:, 0:count, 0, w * HD : (w + 1) * HD]
                )
            totals = work.tile([P, count, 2, HD], F32)
            nc.scalar.copy(
                out=totals[:].rearrange("p i w f -> p i (w f)"), in_=sums[:, 0:count, 1, :]
            )
            swapped_of[first_pair], totals_of[first_pair] = swapped, totals

        def multiply_windows(first_pair):
            swapped = swapped_of[first_pair]
            both = work.tile([P, batch_of[first_pair][1], HD], F32)
            nc.vector.tensor_tensor(
                out=both[:], in0=swapped[:, :, 0], in1=swapped[:, :, 1], op=ALU.mult
            )
            both_of[first_pair] = both

        def multiply_pairs(first_pair):
            both = both_of[first_pair]
            whole = work.tile([P, 1, HD], F32)
            nc.vector.tensor_tensor(out=whole[:, 0], in0=both[:, 0], in1=both[:, 1], op=ALU.mult)
            whole_of[first_pair] = whole

        def invert(first_pair):
            whole = (whole_of if batch_of[first_pair][1] == 2 else both_of)[first_pair]
            inverse = work.tile([P, 1, HD], F32)
            nc.vector.reciprocal(out=inverse[:], in_=whole[:])
            inverse_of[first_pair] = inverse

        def share_inverse(first_pair):
            shared = work.tile([P, 2, HD], F32)
            nc.vector.tensor_tensor(
                out=shared[:], in0=both_of[first_pair][:, ::-1],
                in1=inverse_of[first_pair][:].to_broadcast([P, 2, HD]), op=ALU.mult,
            )
            inverse_of[first_pair] = shared

        def scale_values(first_pair, engine=nc.vector):
            count = batch_of[first_pair][1]
            scaled = work.tile([P, count, 2, HD], F32)
            engine.tensor_tensor(
                out=scaled[:], in0=totals_of[first_pair][:],
                in1=inverse_of[first_pair][:].unsqueeze(2).to_broadcast([P, count, 2, HD]), op=ALU.mult,
            )
            scaled_of[first_pair] = scaled

        def divide(first_pair):
            pooled = work.tile([P, batch_of[first_pair][1], 2, HD], F32)
            nc.vector.tensor_tensor(
                out=pooled[:], in0=scaled_of[first_pair][:], in1=swapped_of[first_pair][:], op=ALU.mult
            )
            pooled_of[first_pair] = pooled

        def invert_each(n):
            inverse = work.tile([P, 2 * HD], F32, tag="inverse_each")
            nc.vector.reciprocal(out=inverse[:], in_=sums_of[n][:, 0, 0, :])
            inverse_of[n] = inverse

        def divide_each(n):
            pooled = work.tile([P, 1, 2, HD], F32)
            pooled_of[n] = pooled
            nc.vector.tensor_tensor(
                out=pooled[:].rearrange("p i w f -> p (i w f)"), in0=sums_of[n][:, 0, 1, :],
                in1=inverse_of[n][:], op=ALU.mult,
            )

        def rows_of(out, first, count):
            return out.rearrange("b w f -> (b w) f").rearrange("(p w) f -> p w f", p=P)[
                :, 2 * first : 2 * (first + count), :
            ]

        def finish(first):
            count = batch_of[first][1]
            size = 2 * count
            pooled = pooled_of[first][:].rearrange("p i w f -> p (i w) f")
            nc.sync.dma_start(out=rows_of(out_1, first, count), in_=pooled)
            nc.sync.dma_start(
                out=rows_of(out_0, first, count)[:, :, 0 : HD - ROPE], in_=pooled[:, :, 0 : HD - ROPE]
            )
            products = work.tile([P, size, 2, HALF, 2], F32)
            engine = nc.vector if first == TWOS - 1 else nc.gpsimd
            for o in range(2):
                engine.tensor_tensor(
                    out=products[:, :, o],
                    in0=pooled[:, :, HD - ROPE : HD].rearrange("p w (j i) -> p w j i", i=2),
                    in1=table[:, 2 * first : 2 * first + size, o]
                    .unsqueeze(3)
                    .to_broadcast([P, size, HALF, 2]),
                    op=ALU.mult,
                )
            rotated = work.tile([P, size, ROPE], F32)
            pairs = rotated[:].rearrange("p w (j i) -> p w j i", i=2)
            for i, op in ((0, ALU.subtract), (1, ALU.add)):
                engine.tensor_tensor(
                    out=pairs[:, :, :, i],
                    in0=products[:, :, 0, :, i],
                    in1=products[:, :, 1, :, 1 - i],
                    op=op,
                )
            nc.sync.dma_start(
                out=rows_of(out_0, first, count)[:, :, HD - ROPE : HD], in_=rotated[:]
            )

        def pair(n):
            return n if 0 <= n < TWOS else None

        def flip_and_group(i):
            for half in range(2):
                flip_words(i, half)
                group_words(i, half)

        keep_warm(WARM_UPS)
        turn_pieces[0]()
        flip_and_group(0)
        turn_pieces[1]()
        quantise(0)
        flip_and_group(1)
        flip_and_group(2)
        spread_ape()
        table_pieces[0]()
        flip_words(3, 0)
        group_words(3, 0)
        flip_words(3, 1)
        table_pieces[1]()
        table_pieces[2]()
        weights = group_weights(nc, const, raw)
        move_on()
        quantise_weights(nc, weights, w_codes, w_scales)
        quantise(1)
        quantise(2)
        group_words(3, 1, nc.vector.tensor_copy)
        turn_ape()
        flip_words(4, 0)
        group_words(4, 0)
        flip_words(4, 1)
        project(0, 0, 0)
        project(0, 0, 1)
        quantise(3)
        land(0, 0)
        group_words(4, 1, nc.vector.tensor_copy)
        land(0, 1)
        nc.scalar.activation(out=nothing[:], in_=nothing[:], func=ACT.Exp)
        for i in range(5):
            load(i + LOADS)

        for k in range(TWOS):
            landing, coming, exped, weighed = pair(k), pair(k + 1), pair(k - 1), pair(k - 2)
            flips = [i for i in (2 * k + 5, 2 * k + 6) if i < UNITS]
            quantised = [i for i in (2 * k + 4, 2 * k + 5) if i < UNITS]
            summed = pair(k - 3)
            divided = pair(k - 5) if k % 2 == 1 else None
            finished = pair(k - 6) if k % 2 == 0 else None

            if divided is not None:
                keep_sums(divided)
            if landing > 0:
                land(landing, 0)
                land(landing, 1)
            if exped is not None:
                subtract_top(exped)
            if divided is not None:
                multiply_windows(divided)
            if quantised:
                quantise(quantised[0])
            if divided is not None:
                multiply_pairs(divided)
            if divided is not None:
                invert(divided)
            top_of_4(landing)
            if divided is not None:
                share_inverse(divided)
                scale_values(divided, nc.gpsimd)
            if finished is not None:
                divide(finished)
            if flips:
                flip_words(flips[0], 0)
                flip_words(flips[0], 1)
                group_words(flips[0], 0)
                if k >= 2:
                    group_words(flips[0], 1)
            if weighed is not None:
                project(weighed, 1, 0)
            if coming is not None:
                project(coming, 0, 0)
            if summed is not None:
                add_slots(summed, 0)
                add_slots(summed, 1)
            if len(flips) > 1:
                flip_words(flips[1], 0)
                flip_words(flips[1], 1)
            if coming is not None:
                project(coming, 0, 1)
            if weighed is not None:
                weigh(weighed, 1)
            top_of_2(landing)
            if weighed is not None:
                weigh(weighed, 0)
            top_of_1(landing)
            if exped is not None:
                project(exped, 1, 1)
            if k < 2:
                group_words(flips[0], 1, nc.vector.tensor_copy)
            if len(quantised) > 1:
                quantise(quantised[1])
            if exped is not None:
                exponentiate(exped, 0)
                exponentiate(exped, 1)
            if len(flips) > 1:
                group_words(flips[1], 0)
                group_words(flips[1], 1)
            if finished is not None:
                finish(finished)
            for i in flips:
                if i + LOADS < UNITS:
                    load(i + LOADS)

        last = TWOS - 1
        add_slots(last - 2, 0)
        add_slots(last - 2, 1)
        project(last - 1, 1, 0)
        project(last, 1, 1)
        project(last, 1, 0)
        subtract_top(last)
        exponentiate(last, 1)
        exponentiate(last, 0)
        weigh(last - 1, 1)
        divide(last - 5)
        finish(last - 5)
        weigh(last - 1, 0)
        keep_sums(last - 3)
        add_slots(last - 1, 0)
        add_slots(last - 1, 1)
        multiply_windows(last - 3)
        weigh(last, 1)
        multiply_pairs(last - 3)
        weigh(last, 0)
        invert(last - 3)
        keep_sums(last - 1)
        add_slots(last, 0)
        add_slots(last, 1)
        share_inverse(last - 3)
        multiply_windows(last - 1)
        scale_values(last - 3)
        invert(last - 1)
        divide(last - 3)
        finish(last - 3)
        scale_values(last - 1)
        invert_each(last)
        divide(last - 1)
        finish(last - 1)
        divide_each(last)
        finish(last)
